import numpy as np
import ml_dtypes


def mxq(x, axis, fmt="e4m3"):
    dtype, down = {"e4m3": (ml_dtypes.float8_e4m3fn, 7), "e5m2": (ml_dtypes.float8_e5m2, 14)}[fmt]
    v = np.moveaxis(np.asarray(x, np.float32).astype(ml_dtypes.bfloat16).astype(np.float64), axis, -1)
    blocks = v.reshape(v.shape[:-1] + (-1, 32))
    amax = np.abs(blocks).max(-1, keepdims=True)
    byte = np.maximum(np.where(amax > 0, np.frexp(amax)[1] - 1 + 127, 0) - down, 1)
    scale = np.exp2(byte - 127.0)
    codes = (blocks / scale).astype(np.float32).astype(dtype).astype(np.float64)
    return np.moveaxis((codes * scale).reshape(v.shape), -1, axis)


WIDE = False


def mx_kscale(k):
    if not WIDE:
        return np.ones(k)
    levels = np.array([10, -10, 5, -5, 0])
    a = np.random.permutation(np.resize(levels, k // 512 * 4)).reshape(k // 512, 4)
    idx = np.arange(k)
    return np.exp2(a[idx // 512, idx % 128 // 32])


BF16 = ml_dtypes.bfloat16


def bf(x):
    return np.asarray(x, np.float32).astype(BF16)


def f64(x):
    return np.asarray(x).astype(np.float64)


E2M1 = np.array([0.0, 0.5, 1.0, 1.5, 2.0, 3.0, 4.0, 6.0, -0.0, -0.5, -1.0, -1.5, -2.0, -3.0, -4.0, -6.0])


def pack_weight(w, fmt):
    k, n = w.shape
    w = f64(bf(w)).reshape(k // 32, 32, n)
    amax = np.abs(w).max(1)
    if fmt == "e4m3":
        byte = np.frexp(amax)[1] - 1 + 127 - 7
    else:
        mant, ex = np.frexp(amax / 6.0)
        byte = np.where(mant > 0.5, ex, ex - 1) + 127
    byte = np.clip(np.where(amax > 0, byte, 1), 1, 254)
    scaled = (w * np.exp2(127.0 - byte)[:, None, :]).reshape(k, n).astype(np.float32)
    by_word = np.ascontiguousarray(scaled.reshape(k // 512, 128, 4, n).transpose(0, 1, 3, 2))
    if fmt == "e4m3":
        words = by_word.astype(ml_dtypes.float8_e4m3fn).view(np.uint8)
    else:
        c = by_word.astype(ml_dtypes.float4_e2m1fn).view(np.uint8) & 0xF
        words = c[..., 0::2] | (c[..., 1::2] << 4)
    return np.ascontiguousarray(words), np.ascontiguousarray(byte.astype(np.uint8).reshape(k // 512, 16, n))


def unpack_weight(words, scales, fmt):
    g, p, n, _ = words.shape
    if fmt == "e4m3":
        vals = np.ascontiguousarray(words).view(ml_dtypes.float8_e4m3fn).astype(np.float64)
    else:
        nib = np.empty((g, p, n, 4), np.uint8)
        nib[..., 0::2] = words & 0xF
        nib[..., 1::2] = words >> 4
        vals = E2M1[nib]
    vals = vals * np.repeat(np.exp2(scales.astype(np.float64) - 127.0), 8, axis=1)[..., None]
    return vals.transpose(0, 1, 3, 2).reshape(g * 512, n)


NP, NH, NF, NU, B, C, H, W, IN_DIM = 7, 3, 2, 4, 8, 512, 8, 16, 256
NL = NP - 1 - NU
S = H * W
EPS = 1e-5
FMT = "e4m3"


def make_bn():
    return bf(np.stack([1.0 + 0.1 * np.random.standard_normal(C), 0.1 * np.random.standard_normal(C),
                        0.1 * np.random.standard_normal(C), np.random.uniform(0.5, 1.5, C)]))


def make_w(col):
    w = np.random.standard_normal((C, col.size)) / np.sqrt(col.size) / col
    return pack_weight(np.ascontiguousarray(w.T), FMT)


def make_nodes(n, s):
    return bf(np.random.standard_normal((n, B, C, H, W)) * s[:, None, None])


def setup_inputs():
    s = mx_kscale(C)
    p_nodes = make_nodes(NP, s)
    h_nodes = make_nodes(NH, s)
    f_nodes = make_nodes(NF, s)
    wd_words, wd_scales = make_w(np.concatenate([s, s]))
    bn_d = make_bn()
    wu_words, wu_scales = make_w(np.concatenate([np.repeat(s, NU), s]))
    bn_u = make_bn()
    wl_words, wl_scales = make_w(np.concatenate([np.repeat(s, NL), s]))
    bn_l = make_bn()
    wb_words, wb_scales = make_w(np.concatenate([s, s, s]))
    bn_b = make_bn()
    return {'p_nodes': p_nodes, 'h_nodes': h_nodes, 'f_nodes': f_nodes,
            'W_decomp_full_words': wd_words, 'W_decomp_full_scales': wd_scales, 'bn_decomp_full': bn_d,
            'W_comp_u_words': wu_words, 'W_comp_u_scales': wu_scales, 'bn_comp_u': bn_u,
            'W_comp_l_words': wl_words, 'W_comp_l_scales': wl_scales, 'bn_comp_l': bn_l,
            'W_bg_h_words': wb_words, 'W_bg_h_scales': wb_scales, 'bn_bg_h': bn_b}


def conv(wq, xs):
    y, c0 = 0.0, 0
    for x in xs:
        c1 = c0 + x.shape[1]
        y = y + (wq[:, c0:c1] @ x)
        c0 = c1
    return y


def bn_relu(y, bn):
    gamma, beta, mean, var = f64(bn)
    scale = gamma / np.sqrt(var + EPS)
    shift = beta - mean * scale
    return np.maximum(y * scale[:, None] + shift[:, None], 0.0)


def reference(p_nodes, h_nodes, f_nodes, W_decomp_full_words, W_decomp_full_scales, bn_decomp_full,
              W_comp_u_words, W_comp_u_scales, bn_comp_u, W_comp_l_words, W_comp_l_scales, bn_comp_l,
              W_bg_h_words, W_bg_h_scales, bn_bg_h):
    p = f64(p_nodes).reshape(NP, B, C, S)
    upper = np.moveaxis(p[1:1 + NU], 0, 2).reshape(B, NU * C, S)
    lower = np.moveaxis(p[1 + NU:], 0, 2).reshape(B, NL * C, S)
    fq = mxq(f64(f_nodes).reshape(NF, B, C, S), 2, 'e4m3')
    hq = mxq(f64(h_nodes).reshape(NH, B, C, S), 2, 'e4m3')
    p0q = mxq(p[0], 1, 'e4m3')
    uq = mxq(upper, 1, 'e4m3')
    lq = mxq(lower, 1, 'e4m3')
    wd = unpack_weight(W_decomp_full_words, W_decomp_full_scales, FMT).T
    wu = unpack_weight(W_comp_u_words, W_comp_u_scales, FMT).T
    wl = unpack_weight(W_comp_l_words, W_comp_l_scales, FMT).T
    wb = unpack_weight(W_bg_h_words, W_bg_h_scales, FMT).T
    h0 = bn_relu(conv(wb, [fq[0], hq[0], p0q]), bn_bg_h)
    h1 = bn_relu(conv(wu, [uq, hq[1]]), bn_comp_u) + bn_relu(conv(wd, [fq[1], hq[1]]), bn_decomp_full)
    h2 = bn_relu(conv(wl, [lq, hq[2]]), bn_comp_l) + bn_relu(conv(wd, [fq[1], hq[2]]), bn_decomp_full)
    return np.stack([h0, h1, h2]).reshape(NH, B, C, H, W)

@@ -1,0 +1,231 @@
+from contextlib import ExitStack
+
+import concourse.mybir as mybir
+from concourse.masks import make_identity
+
+F32 = mybir.dt.float32
+BF16 = mybir.dt.bfloat16
+I32 = mybir.dt.int32
+U32 = mybir.dt.uint32
+U8 = mybir.dt.uint8
+FP8X4 = mybir.dt.float8_e4m3fn_x4
+RELU = mybir.ActivationFunctionType.Relu
+
+P = 128
+PACK = 4
+BATCH = 8
+CHANNELS = 512
+PIXELS = 128
+O_TILES = CHANNELS // P
+CHUNK_BATCHES = 4
+CHUNKS = BATCH // CHUNK_BATCHES
+CHUNK_COLS = CHUNK_BATCHES * PIXELS
+NODE_PASSES = 12
+QUADRANTS = 4
+LIVE_ROWS = 4
+VECTOR_PIXELS = 96
+EPS = 1e-5
+BN_ROWS = 4
+
+FLOPS = 2 * CHANNELS * (1536 + 2560 + 1536 + 1024 + 1024) * BATCH * PIXELS
+
+
+def tile_gnn_pa_kernel(
+    tc,
+    p_nodes,
+    h_nodes,
+    f_nodes,
+    W_decomp_full_words,
+    W_decomp_full_scales,
+    bn_decomp_full,
+    W_comp_u_words,
+    W_comp_u_scales,
+    bn_comp_u,
+    W_comp_l_words,
+    W_comp_l_scales,
+    bn_comp_l,
+    W_bg_h_words,
+    W_bg_h_scales,
+    bn_bg_h,
+    out,
+):
+    nc = tc.nc
+    parts = p_nodes.rearrange("n b c y x -> n b c (y x)")
+    halves = h_nodes.rearrange("n b c y x -> n b c (y x)")
+    fulls = f_nodes.rearrange("n b c y x -> n b c (y x)")
+    result = out.rearrange("n b c y x -> n b c (y x)")
+
+    groups = {
+        "upper": (parts[1], parts[2], parts[3], parts[4]),
+        "half1": (halves[1],),
+        "full1": (fulls[1],),
+        "lower": (parts[5], parts[6]),
+        "half2": (halves[2],),
+        "full0": (fulls[0],),
+        "half0": (halves[0],),
+        "part0": (parts[0],),
+    }
+    first_pass = {}
+    passes_so_far = 0
+    for name in groups:
+        first_pass[name] = passes_so_far
+        passes_so_far += len(groups[name])
+    assert passes_so_far == NODE_PASSES
+
+    convolutions = {
+        "comp_u": (W_comp_u_words, W_comp_u_scales, bn_comp_u),
+        "decomp": (W_decomp_full_words, W_decomp_full_scales, bn_decomp_full),
+        "comp_l": (W_comp_l_words, W_comp_l_scales, bn_comp_l),
+        "bg": (W_bg_h_words, W_bg_h_scales, bn_bg_h),
+    }
+    conv_names = list(convolutions)
+    weights_behind = {"half1": "comp_u", "full1": "decomp", "half2": "comp_l", "part0": "bg"}
+
+    with ExitStack() as ctx:
+        keep = ctx.enter_context(tc.tile_pool(name="keep", bufs=1))
+        stage = ctx.enter_context(tc.tile_pool(name="stage", bufs=3))
+        psum = ctx.enter_context(tc.psum_pool(name="psum", bufs=8))
+
+        w_words = {}
+        w_planes = {}
+        for conv in conv_names:
+            passes = convolutions[conv][0].shape[0]
+            w_words[conv] = keep.tile([P, passes, CHANNELS], I32, name="words_" + conv, align_bytes=64)
+            w_planes[conv] = keep.tile([P, passes, CHANNELS], U8, name="planes_" + conv, align_bytes=64)
+            nc.vector.memset(w_planes[conv][:].bitcast(I32), 0)
+
+        def load_weights(conv):
+            words, scales = convolutions[conv][0], convolutions[conv][1]
+            for quadrant in range(QUADRANTS):
+                nc.sync.dma_start(
+                    out=w_planes[conv][32 * quadrant : 32 * quadrant + LIVE_ROWS].bitcast(I32),
+                    in_=scales[:, LIVE_ROWS * quadrant : LIVE_ROWS * (quadrant + 1), :]
+                    .rearrange("g r n -> r g n")
+                    .bitcast(I32),
+                )
+            nc.sync.dma_start(out=w_words[conv][:], in_=words.rearrange("g p n t -> p g (n t)").bitcast(I32))
+
+        def load_group(name, chunk):
+            nodes = groups[name]
+            n = len(nodes)
+            raw = keep.tile(
+                [P, n, CHUNK_BATCHES, n, (PACK // n) * PIXELS], BF16, name="raw_%s_%d" % (name, chunk)
+            )
+            for j in range(n):
+                nc.sync.dma_start(
+                    out=raw[:, j],
+                    in_=nodes[j][chunk * CHUNK_BATCHES : (chunk + 1) * CHUNK_BATCHES].rearrange(
+                        "b (g p e) s -> p b g (e s)", g=n, p=P
+                    ),
+                )
+            return raw
+
+        raws = {}
+        for chunk in range(CHUNKS):
+            for name in groups:
+                raws[name, chunk] = load_group(name, chunk)
+                if chunk == 0 and name in weights_behind:
+                    load_weights(weights_behind[name])
+
+        bn_rows = keep.tile([P, P], BF16, name="bn_rows")
+        nc.vector.memset(bn_rows[P // 2 :, :], 0.0)
+        rows_per_bn = BN_ROWS * O_TILES
+        for i in range(len(conv_names)):
+            nc.scalar.dma_start(
+                out=bn_rows[i * rows_per_bn : (i + 1) * rows_per_bn, :],
+                in_=convolutions[conv_names[i]][2].rearrange("r (j m) -> (r j) m", m=P),
+            )
+        identity = keep.tile([P, P], BF16, name="identity")
+        make_identity(nc, identity[:])
+        bn_turned = psum.tile([P, P], BF16, name="bn_turned", tag="acc")
+        nc.tensor.transpose(bn_turned[:], bn_rows[:], identity[:])
+        bn_cols = keep.tile([P, len(conv_names), BN_ROWS, O_TILES], F32, name="bn_cols")
+        nc.vector.tensor_copy(
+            out=bn_cols[:].rearrange("p i r j -> p (i r j)"), in_=bn_turned[:, : len(conv_names) * rows_per_bn]
+        )
+        gamma, beta, mean, var = [bn_cols[:, :, r, :] for r in range(BN_ROWS)]
+        bn_scale = keep.tile([P, len(conv_names), O_TILES], F32, name="bn_scale")
+        bn_shift = keep.tile([P, len(conv_names), O_TILES], F32, name="bn_shift")
+        nc.vector.tensor_scalar_add(out=bn_scale[:], in0=var, scalar1=EPS)
+        nc.scalar.sqrt(out=bn_scale[:], in_=bn_scale[:])
+        nc.vector.reciprocal(out=bn_scale[:], in_=bn_scale[:])
+        nc.vector.tensor_mul(out=bn_scale[:], in0=bn_scale[:], in1=gamma)
+        nc.vector.tensor_mul(out=bn_shift[:], in0=mean, in1=bn_scale[:])
+        nc.vector.tensor_sub(out=bn_shift[:], in0=beta, in1=bn_shift[:])
+
+        def quantise_group(name, chunk, codes, planes):
+            raw = raws[name, chunk]
+            n = len(groups[name])
+            for g in range(n):
+                grouped = stage.tile([P, CHUNK_BATCHES, PIXELS, PACK], BF16, name="grouped", align_bytes=64)
+                source = raw[:, :, :, g, :].rearrange("p j b (e s) -> p b s e j", s=PIXELS)
+                target = grouped[:].rearrange("p b s (e j) -> p b s e j", j=n)
+                if n == 2:
+                    nc.vector.tensor_copy(out=target, in_=source)
+                else:
+                    nc.vector.tensor_copy(out=target[:, :, :VECTOR_PIXELS], in_=source[:, :, :VECTOR_PIXELS])
+                    nc.scalar.copy(out=target[:, :, VECTOR_PIXELS:], in_=source[:, :, VECTOR_PIXELS:])
+                nc.vector.quantize_mx(
+                    out=codes[:, first_pass[name] + g, :].bitcast(FP8X4),
+                    scales=planes[:, first_pass[name] + g, :],
+                    in_=grouped[:].rearrange("p b s t -> p (b s t)"),
+                )
+
+        def convolve(conv, names, codes, planes):
+            feature_passes = [first_pass[name] + g for name in names for g in range(len(groups[name]))]
+            accs = [psum.tile([P, CHUNK_COLS], F32, name="acc", tag="acc") for o in range(O_TILES)]
+            for k in range(len(feature_passes)):
+                for o in range(O_TILES):
+                    nc.tensor.matmul_mx(
+                        out=accs[o][:],
+                        lhsT=w_words[conv][:, k, o * P : (o + 1) * P].bitcast(FP8X4),
+                        lhsT_scale=w_planes[conv][:, k, o * P : (o + 1) * P],
+                        rhs=codes[:, feature_passes[k], :].bitcast(FP8X4),
+                        rhs_scale=planes[:, feature_passes[k], :],
+                        start=(k == 0),
+                        stop=(k == len(feature_passes) - 1),
+                    )
+            return accs
+
+        def norm_relu(conv, o, acc, tag):
+            i = conv_names.index(conv)
+            branch = stage.tile([P, CHUNK_BATCHES, PIXELS], F32, name=tag, tag=tag)
+            nc.scalar.activation(
+                out=branch[:].rearrange("p b s -> p (b s)"),
+                in_=acc[:],
+                func=RELU,
+                bias=bn_shift[:, i, o : o + 1],
+                scale=bn_scale[:, i, o : o + 1],
+            )
+            return branch
+
+        def store(half, chunk, o, values):
+            nc.scalar.dma_start(
+                out=result[
+                    half, chunk * CHUNK_BATCHES : (chunk + 1) * CHUNK_BATCHES, o * P : (o + 1) * P, :
+                ].rearrange("b m s -> m b s"),
+                in_=values[:],
+            )
+
+        for chunk in range(CHUNKS):
+            codes = keep.tile([P, NODE_PASSES, CHUNK_COLS], U32, name="codes_%d" % chunk, align_bytes=64)
+            planes = keep.tile([P, NODE_PASSES, CHUNK_COLS], U8, name="planes_%d" % chunk, align_bytes=64)
+
+            for half, conv, own, half_name in ((1, "comp_u", "upper", "half1"), (2, "comp_l", "lower", "half2")):
+                quantise_group(own, chunk, codes, planes)
+                quantise_group(half_name, chunk, codes, planes)
+                if half == 1:
+                    quantise_group("full1", chunk, codes, planes)
+                composed = convolve(conv, (own, half_name), codes, planes)
+                decomposed = convolve("decomp", ("full1", half_name), codes, planes)
+                for o in range(O_TILES):
+                    total = norm_relu(conv, o, composed[o], "total")
+                    other = norm_relu("decomp", o, decomposed[o], "other")
+                    nc.vector.tensor_add(out=total[:], in0=total[:], in1=other[:])
+                    store(half, chunk, o, total)
+
+            for name in ("full0", "half0", "part0"):
+                quantise_group(name, chunk, codes, planes)
+            background = convolve("bg", ("full0", "half0", "part0"), codes, planes)
+            for o in range(O_TILES):
+                store(0, chunk, o, norm_relu("bg", o, background[o], "total"))

@@ -23,7 +23,6 @@ CHUNK_COLS = CHUNK_BATCHES * PIXELS
 NODE_PASSES = 12
 QUADRANTS = 4
 LIVE_ROWS = 4
-VECTOR_PIXELS = 96
 EPS = 1e-5
 BN_ROWS = 4
 
@@ -56,14 +55,14 @@ def tile_gnn_pa_kernel(
     result = out.rearrange("n b c y x -> n b c (y x)")
 
     groups = {
-        "upper": (parts[1], parts[2], parts[3], parts[4]),
-        "half1": (halves[1],),
-        "full1": (fulls[1],),
-        "lower": (parts[5], parts[6]),
-        "half2": (halves[2],),
         "full0": (fulls[0],),
         "half0": (halves[0],),
         "part0": (parts[0],),
+        "full1": (fulls[1],),
+        "half1": (halves[1],),
+        "half2": (halves[2],),
+        "lower": (parts[5], parts[6]),
+        "upper": (parts[1], parts[2], parts[3], parts[4]),
     }
     first_pass = {}
     passes_so_far = 0
@@ -73,17 +72,23 @@ def tile_gnn_pa_kernel(
     assert passes_so_far == NODE_PASSES
 
     convolutions = {
-        "comp_u": (W_comp_u_words, W_comp_u_scales, bn_comp_u),
+        "bg": (W_bg_h_words, W_bg_h_scales, bn_bg_h),
         "decomp": (W_decomp_full_words, W_decomp_full_scales, bn_decomp_full),
         "comp_l": (W_comp_l_words, W_comp_l_scales, bn_comp_l),
-        "bg": (W_bg_h_words, W_bg_h_scales, bn_bg_h),
+        "comp_u": (W_comp_u_words, W_comp_u_scales, bn_comp_u),
     }
     conv_names = list(convolutions)
-    weights_behind = {"half1": "comp_u", "full1": "decomp", "half2": "comp_l", "part0": "bg"}
+
+    node_stages = (
+        (0, "bg", ("full0", "half0", "part0"), None),
+        (2, "comp_l", ("lower",), "half2"),
+        (1, "comp_u", ("upper",), "half1"),
+    )
+    stages = [(0,) + s for s in node_stages] + [(1,) + s for s in reversed(node_stages)]
 
     with ExitStack() as ctx:
         keep = ctx.enter_context(tc.tile_pool(name="keep", bufs=1))
-        stage = ctx.enter_context(tc.tile_pool(name="stage", bufs=3))
+        stage_pool = ctx.enter_context(tc.tile_pool(name="stage", bufs=4))
         psum = ctx.enter_context(tc.psum_pool(name="psum", bufs=8))
 
         w_words = {}
@@ -121,11 +126,20 @@ def tile_gnn_pa_kernel(
             return raw
 
         raws = {}
-        for chunk in range(CHUNKS):
-            for name in groups:
-                raws[name, chunk] = load_group(name, chunk)
-                if chunk == 0 and name in weights_behind:
-                    load_weights(weights_behind[name])
+        loaded_weights = set()
+
+        def load_step(chunk, names, conv):
+            for name in names:
+                if (name, chunk) not in raws:
+                    raws[name, chunk] = load_group(name, chunk)
+                if conv not in loaded_weights:
+                    load_weights(conv)
+                    loaded_weights.add(conv)
+
+        for chunk, node, conv, own, half in stages:
+            if half is not None:
+                load_step(chunk, (half, "full1"), "decomp")
+            load_step(chunk, own, conv)
 
         bn_rows = keep.tile([P, P], BF16, name="bn_rows")
         nc.vector.memset(bn_rows[P // 2 :, :], 0.0)
@@ -153,79 +167,99 @@ def tile_gnn_pa_kernel(
         nc.vector.tensor_mul(out=bn_shift[:], in0=mean, in1=bn_scale[:])
         nc.vector.tensor_sub(out=bn_shift[:], in0=beta, in1=bn_shift[:])
 
-        def quantise_group(name, chunk, codes, planes):
-            raw = raws[name, chunk]
+        codes = [
+            keep.tile([P, NODE_PASSES, CHUNK_COLS], U32, name="codes_%d" % chunk, align_bytes=64)
+            for chunk in range(CHUNKS)
+        ]
+        planes = [
+            keep.tile([P, NODE_PASSES, CHUNK_COLS], U8, name="planes_%d" % chunk, align_bytes=64)
+            for chunk in range(CHUNKS)
+        ]
+        quantised = set()
+
+        def quantise_group(name, chunk):
+            if (name, chunk) in quantised:
+                return
+            quantised.add((name, chunk))
             n = len(groups[name])
             for g in range(n):
-                grouped = stage.tile([P, CHUNK_BATCHES, PIXELS, PACK], BF16, name="grouped", align_bytes=64)
-                source = raw[:, :, :, g, :].rearrange("p j b (e s) -> p b s e j", s=PIXELS)
-                target = grouped[:].rearrange("p b s (e j) -> p b s e j", j=n)
-                if n == 2:
-                    nc.vector.tensor_copy(out=target, in_=source)
-                else:
-                    nc.vector.tensor_copy(out=target[:, :, :VECTOR_PIXELS], in_=source[:, :, :VECTOR_PIXELS])
-                    nc.scalar.copy(out=target[:, :, VECTOR_PIXELS:], in_=source[:, :, VECTOR_PIXELS:])
+                grouped = stage_pool.tile([P, CHUNK_BATCHES, PIXELS, PACK], BF16, name="grouped", align_bytes=64)
+                nc.vector.tensor_copy(
+                    out=grouped[:].rearrange("p b s (e j) -> p b s e j", j=n),
+                    in_=raws[name, chunk][:, :, :, g, :].rearrange("p j b (e s) -> p b s e j", s=PIXELS),
+                )
                 nc.vector.quantize_mx(
-                    out=codes[:, first_pass[name] + g, :].bitcast(FP8X4),
-                    scales=planes[:, first_pass[name] + g, :],
+                    out=codes[chunk][:, first_pass[name] + g, :].bitcast(FP8X4),
+                    scales=planes[chunk][:, first_pass[name] + g, :],
                     in_=grouped[:].rearrange("p b s t -> p (b s t)"),
                 )
 
-        def convolve(conv, names, codes, planes):
-            feature_passes = [first_pass[name] + g for name in names for g in range(len(groups[name]))]
+        def convolve(conv, chunk, concatenation, first_names):
+            pairs = []
+            for name in concatenation:
+                for g in range(len(groups[name])):
+                    pairs.append((name not in first_names, len(pairs), first_pass[name] + g))
+            pairs = sorted(pairs)
             accs = [psum.tile([P, CHUNK_COLS], F32, name="acc", tag="acc") for o in range(O_TILES)]
-            for k in range(len(feature_passes)):
+            for late, k, feature_pass in pairs:
                 for o in range(O_TILES):
                     nc.tensor.matmul_mx(
                         out=accs[o][:],
                         lhsT=w_words[conv][:, k, o * P : (o + 1) * P].bitcast(FP8X4),
                         lhsT_scale=w_planes[conv][:, k, o * P : (o + 1) * P],
-                        rhs=codes[:, feature_passes[k], :].bitcast(FP8X4),
-                        rhs_scale=planes[:, feature_passes[k], :],
-                        start=(k == 0),
-                        stop=(k == len(feature_passes) - 1),
+                        rhs=codes[chunk][:, feature_pass, :].bitcast(FP8X4),
+                        rhs_scale=planes[chunk][:, feature_pass, :],
+                        start=((late, k, feature_pass) == pairs[0]),
+                        stop=((late, k, feature_pass) == pairs[-1]),
                     )
             return accs
 
-        def norm_relu(conv, o, acc, tag):
+        def norm_relu(conv, accs, tag):
             i = conv_names.index(conv)
-            branch = stage.tile([P, CHUNK_BATCHES, PIXELS], F32, name=tag, tag=tag)
-            nc.scalar.activation(
-                out=branch[:].rearrange("p b s -> p (b s)"),
-                in_=acc[:],
-                func=RELU,
-                bias=bn_shift[:, i, o : o + 1],
-                scale=bn_scale[:, i, o : o + 1],
-            )
-            return branch
-
-        def store(half, chunk, o, values):
-            nc.scalar.dma_start(
-                out=result[
-                    half, chunk * CHUNK_BATCHES : (chunk + 1) * CHUNK_BATCHES, o * P : (o + 1) * P, :
-                ].rearrange("b m s -> m b s"),
-                in_=values[:],
-            )
-
-        for chunk in range(CHUNKS):
-            codes = keep.tile([P, NODE_PASSES, CHUNK_COLS], U32, name="codes_%d" % chunk, align_bytes=64)
-            planes = keep.tile([P, NODE_PASSES, CHUNK_COLS], U8, name="planes_%d" % chunk, align_bytes=64)
-
-            for half, conv, own, half_name in ((1, "comp_u", "upper", "half1"), (2, "comp_l", "lower", "half2")):
-                quantise_group(own, chunk, codes, planes)
-                quantise_group(half_name, chunk, codes, planes)
-                if half == 1:
-                    quantise_group("full1", chunk, codes, planes)
-                composed = convolve(conv, (own, half_name), codes, planes)
-                decomposed = convolve("decomp", ("full1", half_name), codes, planes)
-                for o in range(O_TILES):
-                    total = norm_relu(conv, o, composed[o], "total")
-                    other = norm_relu("decomp", o, decomposed[o], "other")
-                    nc.vector.tensor_add(out=total[:], in0=total[:], in1=other[:])
-                    store(half, chunk, o, total)
-
-            for name in ("full0", "half0", "part0"):
-                quantise_group(name, chunk, codes, planes)
-            background = convolve("bg", ("full0", "half0", "part0"), codes, planes)
+            branches = []
             for o in range(O_TILES):
-                store(0, chunk, o, norm_relu("bg", o, background[o], "total"))
+                branch = stage_pool.tile([P, CHUNK_BATCHES, PIXELS], F32, name=tag, tag=tag)
+                nc.scalar.activation(
+                    out=branch[:].rearrange("p b s -> p (b s)"),
+                    in_=accs[o][:],
+                    func=RELU,
+                    bias=bn_shift[:, i, o : o + 1],
+                    scale=bn_scale[:, i, o : o + 1],
+                )
+                branches.append(branch)
+            return branches
+
+        def store(node, chunk, totals):
+            for o in range(O_TILES):
+                nc.scalar.dma_start(
+                    out=result[
+                        node, chunk * CHUNK_BATCHES : (chunk + 1) * CHUNK_BATCHES, o * P : (o + 1) * P, :
+                    ].rearrange("b m s -> m b s"),
+                    in_=totals[o][:],
+                )
+
+        def finish(open_stage):
+            node, chunk, conv, accs, others = open_stage
+            totals = norm_relu(conv, accs, "total")
+            if others is not None:
+                for o in range(O_TILES):
+                    nc.vector.tensor_add(out=totals[o][:], in0=totals[o][:], in1=others[o][:])
+            return node, chunk, totals
+
+        open_stage = None
+        for chunk, node, conv, own, half in stages:
+            decomposed = None
+            if half is not None:
+                quantise_group(half, chunk)
+                quantise_group("full1", chunk)
+                decomposed = convolve("decomp", chunk, ("full1", half), ())
+            finished = finish(open_stage) if open_stage is not None else None
+            others = norm_relu("decomp", decomposed, "other") if half is not None else None
+            if finished is not None:
+                store(*finished)
+            for name in own:
+                quantise_group(name, chunk)
+            concatenation = own + ((half,) if half is not None else ())
+            accs = convolve(conv, chunk, concatenation, (half,))
+            open_stage = (node, chunk, conv, accs, others)
+        store(*finish(open_stage))

@@ -23,6 +23,8 @@ CHUNK_COLS = CHUNK_BATCHES * PIXELS
 NODE_PASSES = 12
 QUADRANTS = 4
 LIVE_ROWS = 4
+UPPER_PARTS = 4
+ROW_CHANNELS = CHUNK_BATCHES * CHANNELS // P
 EPS = 1e-5
 BN_ROWS = 4
 
@@ -125,6 +127,17 @@ def tile_gnn_pa_kernel(
                 )
             return raw
 
+        def load_upper(chunk):
+            raw = keep.tile([P, UPPER_PARTS, ROW_CHANNELS, PIXELS], BF16, name="raw_upper_%d" % chunk)
+            for j in range(UPPER_PARTS):
+                nc.sync.dma_start(
+                    out=raw[:, j].rearrange("q l s -> q (l s)"),
+                    in_=groups["upper"][j][chunk * CHUNK_BATCHES : (chunk + 1) * CHUNK_BATCHES].rearrange(
+                        "b (h l) s -> (b h) (l s)", l=ROW_CHANNELS
+                    ),
+                )
+            return raw
+
         raws = {}
         loaded_weights = set()
 
@@ -136,7 +149,10 @@ def tile_gnn_pa_kernel(
                     load_weights(conv)
                     loaded_weights.add(conv)
 
-        for chunk, node, conv, own, half in stages:
+        for i in range(len(stages)):
+            chunk, node, conv, own, half = stages[i]
+            if i < CHUNKS:
+                raws["upper", i] = load_upper(i)
             if half is not None:
                 load_step(chunk, (half, "full1"), "decomp")
             load_step(chunk, own, conv)
@@ -151,7 +167,9 @@ def tile_gnn_pa_kernel(
             )
         identity = keep.tile([P, P], BF16, name="identity")
         make_identity(nc, identity[:])
-        bn_turned = psum.tile([P, P], BF16, name="bn_turned", tag="acc")
+        identity_words = keep.tile([P, P], F32, name="identity_words")
+        make_identity(nc, identity_words[:])
+        bn_turned = psum.tile([P, P], BF16, name="bn_turned", tag="bank")
         nc.tensor.transpose(bn_turned[:], bn_rows[:], identity[:])
         bn_cols = keep.tile([P, len(conv_names), BN_ROWS, O_TILES], F32, name="bn_cols")
         nc.vector.tensor_copy(
@@ -176,6 +194,46 @@ def tile_gnn_pa_kernel(
             for chunk in range(CHUNKS)
         ]
         quantised = set()
+        by_pixels = {}
+
+        def turn_upper(chunk):
+            raw = raws["upper", chunk]
+            by_pixel = keep.tile(
+                [P, CHUNK_BATCHES, UPPER_PARTS, 2, P, 2], BF16, name="by_pixel", tag="by_pixel"
+            )
+            quads = ROW_CHANNELS // 4
+            for u in range(2):
+                for quad in range(quads):
+                    turned = psum.tile([P, 4, 2, P], BF16, name="turned", tag="bank")
+                    for l in range(4):
+                        for e in range(2):
+                            nc.tensor.transpose(turned[:, l, e, :], raw[:, 2 * u + e, 4 * quad + l, :], identity[:])
+                    nc.scalar.copy(
+                        out=by_pixel[:, :, :, u].rearrange(
+                            "s b g (h quad l) e -> s (b g) h quad (l e)", quad=quads, l=4
+                        )[:, :, :, quad, :],
+                        in_=turned[:].rearrange("s l e (bg h) -> s bg h (l e)", h=P // ROW_CHANNELS),
+                    )
+            return by_pixel
+
+        def turn_back(by_pixel, g, grouped):
+            words = grouped[:].rearrange("p b s t -> p (b s t)").bitcast(F32)
+            for pair in range(CHUNK_BATCHES // 2):
+                back = psum.tile([P, 2, 2, PIXELS], F32, name="back", tag="bank")
+                for u in range(2):
+                    for b in range(2):
+                        nc.tensor.transpose(
+                            back[:, u, b, :],
+                            by_pixel[:, 2 * pair + b, g, u].rearrange("s p e -> s (p e)").bitcast(F32),
+                            identity_words[:],
+                        )
+                copy_out = nc.scalar.copy if pair == 0 else nc.vector.tensor_copy
+                copy_out(
+                    out=words[:, pair * PIXELS * 4 : (pair + 1) * PIXELS * 4].rearrange(
+                        "p (b s u) -> p b s u", b=2, u=2
+                    ),
+                    in_=back[:].rearrange("p u b s -> p b s u"),
+                )
 
         def quantise_group(name, chunk):
             if (name, chunk) in quantised:
@@ -183,11 +241,16 @@ def tile_gnn_pa_kernel(
             quantised.add((name, chunk))
             n = len(groups[name])
             for g in range(n):
-                grouped = stage_pool.tile([P, CHUNK_BATCHES, PIXELS, PACK], BF16, name="grouped", align_bytes=64)
-                nc.vector.tensor_copy(
-                    out=grouped[:].rearrange("p b s (e j) -> p b s e j", j=n),
-                    in_=raws[name, chunk][:, :, :, g, :].rearrange("p j b (e s) -> p b s e j", s=PIXELS),
+                grouped = stage_pool.tile(
+                    [P, CHUNK_BATCHES, PIXELS, PACK], BF16, name="grouped", bufs=3, align_bytes=64
                 )
+                if name == "upper":
+                    turn_back(by_pixels[chunk], g, grouped)
+                else:
+                    nc.vector.tensor_copy(
+                        out=grouped[:].rearrange("p b s (e j) -> p b s e j", j=n),
+                        in_=raws[name, chunk][:, :, :, g, :].rearrange("p j b (e s) -> p b s e j", s=PIXELS),
+                    )
                 nc.vector.quantize_mx(
                     out=codes[chunk][:, first_pass[name] + g, :].bitcast(FP8X4),
                     scales=planes[chunk][:, first_pass[name] + g, :],
@@ -200,7 +263,7 @@ def tile_gnn_pa_kernel(
                 for g in range(len(groups[name])):
                     pairs.append((name not in first_names, len(pairs), first_pass[name] + g))
             pairs = sorted(pairs)
-            accs = [psum.tile([P, CHUNK_COLS], F32, name="acc", tag="acc") for o in range(O_TILES)]
+            accs = [psum.tile([P, CHUNK_COLS], F32, name="acc", tag="bank") for o in range(O_TILES)]
             for late, k, feature_pass in pairs:
                 for o in range(O_TILES):
                     nc.tensor.matmul_mx(
@@ -247,14 +310,19 @@ def tile_gnn_pa_kernel(
             return node, chunk, totals
 
         open_stage = None
-        for chunk, node, conv, own, half in stages:
-            decomposed = None
+        for i in range(len(stages)):
+            chunk, node, conv, own, half = stages[i]
+            if 0 < i <= CHUNKS:
+                quantise_group("upper", i - 1)
+            if i < CHUNKS:
+                by_pixels[i] = turn_upper(i)
+            others = None
             if half is not None:
                 quantise_group(half, chunk)
                 quantise_group("full1", chunk)
-                decomposed = convolve("decomp", chunk, ("full1", half), ())
             finished = finish(open_stage) if open_stage is not None else None
-            others = norm_relu("decomp", decomposed, "other") if half is not None else None
+            if half is not None:
+                others = norm_relu("decomp", convolve("decomp", chunk, ("full1", half), ()), "other")
             if finished is not None:
                 store(*finished)
             for name in own:

@@ -20,11 +20,10 @@ O_TILES = CHANNELS // P
 CHUNK_BATCHES = 4
 CHUNKS = BATCH // CHUNK_BATCHES
 CHUNK_COLS = CHUNK_BATCHES * PIXELS
-NODE_PASSES = 12
 QUADRANTS = 4
 LIVE_ROWS = 4
-UPPER_PARTS = 4
-ROW_CHANNELS = CHUNK_BATCHES * CHANNELS // P
+RUN = 4
+RAW_TILES = {1: 12, 2: 2, 4: 2}
 EPS = 1e-5
 BN_ROWS = 4
 
@@ -66,13 +65,6 @@ def tile_gnn_pa_kernel(
         "lower": (parts[5], parts[6]),
         "upper": (parts[1], parts[2], parts[3], parts[4]),
     }
-    first_pass = {}
-    passes_so_far = 0
-    for name in groups:
-        first_pass[name] = passes_so_far
-        passes_so_far += len(groups[name])
-    assert passes_so_far == NODE_PASSES
-
     convolutions = {
         "bg": (W_bg_h_words, W_bg_h_scales, bn_bg_h),
         "decomp": (W_decomp_full_words, W_decomp_full_scales, bn_decomp_full),
@@ -92,6 +84,16 @@ def tile_gnn_pa_kernel(
         keep = ctx.enter_context(tc.tile_pool(name="keep", bufs=1))
         stage_pool = ctx.enter_context(tc.tile_pool(name="stage", bufs=4))
         psum = ctx.enter_context(tc.psum_pool(name="psum", bufs=8))
+        ctx.enter_context(tc.manual_schedule())
+
+        bn_rows = keep.tile([P, P], BF16, name="bn_rows")
+        nc.vector.memset(bn_rows[P // 2 :, :], 0.0)
+        rows_per_bn = BN_ROWS * O_TILES
+        for i in range(len(conv_names)):
+            nc.scalar.dma_start(
+                out=bn_rows[i * rows_per_bn : (i + 1) * rows_per_bn, :],
+                in_=convolutions[conv_names[i]][2].rearrange("r (j m) -> (r j) m", m=P),
+            )
 
         w_words = {}
         w_planes = {}
@@ -100,6 +102,10 @@ def tile_gnn_pa_kernel(
             w_words[conv] = keep.tile([P, passes, CHANNELS], I32, name="words_" + conv, align_bytes=64)
             w_planes[conv] = keep.tile([P, passes, CHANNELS], U8, name="planes_" + conv, align_bytes=64)
             nc.vector.memset(w_planes[conv][:].bitcast(I32), 0)
+
+        warm = keep.tile([P, 1], F32, name="warm")
+        nc.vector.memset(warm[:], 1.0)
+        nc.scalar.sqrt(out=warm[:], in_=warm[:])
 
         def load_weights(conv):
             words, scales = convolutions[conv][0], convolutions[conv][1]
@@ -116,24 +122,17 @@ def tile_gnn_pa_kernel(
             nodes = groups[name]
             n = len(nodes)
             raw = keep.tile(
-                [P, n, CHUNK_BATCHES, n, (PACK // n) * PIXELS], BF16, name="raw_%s_%d" % (name, chunk)
+                [P, n, CHUNK_BATCHES, n, (PACK // n) * PIXELS],
+                BF16,
+                name="raw_%s_%d" % (name, chunk),
+                tag="raw_%d" % n,
+                bufs=RAW_TILES[n],
             )
             for j in range(n):
                 nc.sync.dma_start(
                     out=raw[:, j],
                     in_=nodes[j][chunk * CHUNK_BATCHES : (chunk + 1) * CHUNK_BATCHES].rearrange(
                         "b (g p e) s -> p b g (e s)", g=n, p=P
-                    ),
-                )
-            return raw
-
-        def load_upper(chunk):
-            raw = keep.tile([P, UPPER_PARTS, ROW_CHANNELS, PIXELS], BF16, name="raw_upper_%d" % chunk)
-            for j in range(UPPER_PARTS):
-                nc.sync.dma_start(
-                    out=raw[:, j].rearrange("q l s -> q (l s)"),
-                    in_=groups["upper"][j][chunk * CHUNK_BATCHES : (chunk + 1) * CHUNK_BATCHES].rearrange(
-                        "b (h l) s -> (b h) (l s)", l=ROW_CHANNELS
                     ),
                 )
             return raw
@@ -149,27 +148,14 @@ def tile_gnn_pa_kernel(
                     load_weights(conv)
                     loaded_weights.add(conv)
 
-        for i in range(len(stages)):
-            chunk, node, conv, own, half = stages[i]
-            if i < CHUNKS:
-                raws["upper", i] = load_upper(i)
+        for chunk, node, conv, own, half in stages:
             if half is not None:
                 load_step(chunk, (half, "full1"), "decomp")
             load_step(chunk, own, conv)
 
-        bn_rows = keep.tile([P, P], BF16, name="bn_rows")
-        nc.vector.memset(bn_rows[P // 2 :, :], 0.0)
-        rows_per_bn = BN_ROWS * O_TILES
-        for i in range(len(conv_names)):
-            nc.scalar.dma_start(
-                out=bn_rows[i * rows_per_bn : (i + 1) * rows_per_bn, :],
-                in_=convolutions[conv_names[i]][2].rearrange("r (j m) -> (r j) m", m=P),
-            )
         identity = keep.tile([P, P], BF16, name="identity")
         make_identity(nc, identity[:])
-        identity_words = keep.tile([P, P], F32, name="identity_words")
-        make_identity(nc, identity_words[:])
-        bn_turned = psum.tile([P, P], BF16, name="bn_turned", tag="bank")
+        bn_turned = psum.tile([P, P], BF16, name="bn_turned", tag="acc")
         nc.tensor.transpose(bn_turned[:], bn_rows[:], identity[:])
         bn_cols = keep.tile([P, len(conv_names), BN_ROWS, O_TILES], F32, name="bn_cols")
         nc.vector.tensor_copy(
@@ -185,149 +171,137 @@ def tile_gnn_pa_kernel(
         nc.vector.tensor_mul(out=bn_shift[:], in0=mean, in1=bn_scale[:])
         nc.vector.tensor_sub(out=bn_shift[:], in0=beta, in1=bn_shift[:])
 
-        codes = [
-            keep.tile([P, NODE_PASSES, CHUNK_COLS], U32, name="codes_%d" % chunk, align_bytes=64)
-            for chunk in range(CHUNKS)
-        ]
-        planes = [
-            keep.tile([P, NODE_PASSES, CHUNK_COLS], U8, name="planes_%d" % chunk, align_bytes=64)
-            for chunk in range(CHUNKS)
-        ]
-        quantised = set()
-        by_pixels = {}
+        codes = {}
+        planes = {}
+        for chunk in range(CHUNKS):
+            for name in groups:
+                shape = [P, len(groups[name]), CHUNK_COLS]
+                codes[name, chunk] = keep.tile(shape, U32, name="codes_%s_%d" % (name, chunk), align_bytes=64)
+                planes[name, chunk] = keep.tile(shape, U8, name="planes_%s_%d" % (name, chunk), align_bytes=64)
 
-        def turn_upper(chunk):
-            raw = raws["upper", chunk]
-            by_pixel = keep.tile(
-                [P, CHUNK_BATCHES, UPPER_PARTS, 2, P, 2], BF16, name="by_pixel", tag="by_pixel"
-            )
-            quads = ROW_CHANNELS // 4
-            for u in range(2):
-                for quad in range(quads):
-                    turned = psum.tile([P, 4, 2, P], BF16, name="turned", tag="bank")
-                    for l in range(4):
-                        for e in range(2):
-                            nc.tensor.transpose(turned[:, l, e, :], raw[:, 2 * u + e, 4 * quad + l, :], identity[:])
-                    nc.scalar.copy(
-                        out=by_pixel[:, :, :, u].rearrange(
-                            "s b g (h quad l) e -> s (b g) h quad (l e)", quad=quads, l=4
-                        )[:, :, :, quad, :],
-                        in_=turned[:].rearrange("s l e (bg h) -> s bg h (l e)", h=P // ROW_CHANNELS),
-                    )
-            return by_pixel
-
-        def turn_back(by_pixel, g, grouped):
-            words = grouped[:].rearrange("p b s t -> p (b s t)").bitcast(F32)
-            for pair in range(CHUNK_BATCHES // 2):
-                back = psum.tile([P, 2, 2, PIXELS], F32, name="back", tag="bank")
-                for u in range(2):
-                    for b in range(2):
-                        nc.tensor.transpose(
-                            back[:, u, b, :],
-                            by_pixel[:, 2 * pair + b, g, u].rearrange("s p e -> s (p e)").bitcast(F32),
-                            identity_words[:],
-                        )
-                copy_out = nc.scalar.copy if pair == 0 else nc.vector.tensor_copy
-                copy_out(
-                    out=words[:, pair * PIXELS * 4 : (pair + 1) * PIXELS * 4].rearrange(
-                        "p (b s u) -> p b s u", b=2, u=2
-                    ),
-                    in_=back[:].rearrange("p u b s -> p b s u"),
-                )
-
-        def quantise_group(name, chunk):
-            if (name, chunk) in quantised:
-                return
-            quantised.add((name, chunk))
+        def regroup(name, chunk, g, tag):
             n = len(groups[name])
-            for g in range(n):
-                grouped = stage_pool.tile(
-                    [P, CHUNK_BATCHES, PIXELS, PACK], BF16, name="grouped", bufs=3, align_bytes=64
+            raw = raws[name, chunk][:, :, :, g, :]
+            grouped = stage_pool.tile(
+                [P, CHUNK_BATCHES, PIXELS, PACK], BF16, name=tag, tag=tag, bufs=3, align_bytes=64
+            )
+            if tag == "by_scalar":
+                nc.scalar.copy(
+                    out=grouped[:].rearrange("p b s (e j) -> p b s e j", j=n),
+                    in_=raw.rearrange("p j b (e s) -> p b s e j", s=PIXELS),
                 )
-                if name == "upper":
-                    turn_back(by_pixels[chunk], g, grouped)
+            elif n == 2:
+                nc.vector.tensor_copy(
+                    out=grouped[:].rearrange("p b s (e j) -> p b s e j", j=n),
+                    in_=raw.rearrange("p j b (e s) -> p b s e j", s=PIXELS),
+                )
+            else:
+                nc.vector.tensor_copy(
+                    out=grouped[:].rearrange("p b (c i) (e j) -> p b c e j i", i=RUN, j=n),
+                    in_=raw.rearrange("p j b (e c i) -> p b c e j i", e=PACK // n, i=RUN),
+                )
+            return grouped
+
+        def quantise(grouped, name, chunk, g):
+            nc.vector.quantize_mx(
+                out=codes[name, chunk][:, g, :].bitcast(FP8X4),
+                scales=planes[name, chunk][:, g, :],
+                in_=grouped[:].rearrange("p b s t -> p (b s t)"),
+            )
+
+        def prepare(names, chunk, between):
+            passes = [(name, g) for name in names for g in range(len(groups[name]))]
+            tiles = []
+            for k in range(len(passes) + 1):
+                if k < len(passes):
+                    tiles.append(regroup(passes[k][0], chunk, passes[k][1], "by_vector"))
+                if k == 0:
+                    between()
                 else:
-                    nc.vector.tensor_copy(
-                        out=grouped[:].rearrange("p b s (e j) -> p b s e j", j=n),
-                        in_=raws[name, chunk][:, :, :, g, :].rearrange("p j b (e s) -> p b s e j", s=PIXELS),
-                    )
-                nc.vector.quantize_mx(
-                    out=codes[chunk][:, first_pass[name] + g, :].bitcast(FP8X4),
-                    scales=planes[chunk][:, first_pass[name] + g, :],
-                    in_=grouped[:].rearrange("p b s t -> p (b s t)"),
-                )
+                    quantise(tiles[k - 1], passes[k - 1][0], chunk, passes[k - 1][1])
+
+        seen = set()
+
+        def regroup_shared(stage):
+            chunk, node, conv, own, half = stage
+            tiles = []
+            if half is not None:
+                for name in (half, "full1"):
+                    if (name, chunk) not in seen:
+                        seen.add((name, chunk))
+                        tiles.append((name, regroup(name, chunk, 0, "by_scalar")))
+            return tiles
 
         def convolve(conv, chunk, concatenation, first_names):
             pairs = []
             for name in concatenation:
                 for g in range(len(groups[name])):
-                    pairs.append((name not in first_names, len(pairs), first_pass[name] + g))
+                    pairs.append((name not in first_names, len(pairs), name, g))
             pairs = sorted(pairs)
-            accs = [psum.tile([P, CHUNK_COLS], F32, name="acc", tag="bank") for o in range(O_TILES)]
-            for late, k, feature_pass in pairs:
+            accs = [psum.tile([P, CHUNK_COLS], F32, name="acc", tag="acc") for o in range(O_TILES)]
+            for late, k, name, g in pairs:
                 for o in range(O_TILES):
                     nc.tensor.matmul_mx(
                         out=accs[o][:],
                         lhsT=w_words[conv][:, k, o * P : (o + 1) * P].bitcast(FP8X4),
                         lhsT_scale=w_planes[conv][:, k, o * P : (o + 1) * P],
-                        rhs=codes[chunk][:, feature_pass, :].bitcast(FP8X4),
-                        rhs_scale=planes[chunk][:, feature_pass, :],
-                        start=((late, k, feature_pass) == pairs[0]),
-                        stop=((late, k, feature_pass) == pairs[-1]),
+                        rhs=codes[name, chunk][:, g, :].bitcast(FP8X4),
+                        rhs_scale=planes[name, chunk][:, g, :],
+                        start=((late, k, name, g) == pairs[0]),
+                        stop=((late, k, name, g) == pairs[-1]),
                     )
             return accs
 
-        def norm_relu(conv, accs, tag):
+        def norm_relu(conv, o, acc, branch):
             i = conv_names.index(conv)
-            branches = []
-            for o in range(O_TILES):
-                branch = stage_pool.tile([P, CHUNK_BATCHES, PIXELS], F32, name=tag, tag=tag)
-                nc.scalar.activation(
-                    out=branch[:].rearrange("p b s -> p (b s)"),
-                    in_=accs[o][:],
-                    func=RELU,
-                    bias=bn_shift[:, i, o : o + 1],
-                    scale=bn_scale[:, i, o : o + 1],
-                )
-                branches.append(branch)
-            return branches
+            nc.scalar.activation(
+                out=branch.rearrange("p b s -> p (b s)"),
+                in_=acc[:],
+                func=RELU,
+                bias=bn_shift[:, i, o : o + 1],
+                scale=bn_scale[:, i, o : o + 1],
+            )
 
-        def store(node, chunk, totals):
-            for o in range(O_TILES):
-                nc.scalar.dma_start(
-                    out=result[
-                        node, chunk * CHUNK_BATCHES : (chunk + 1) * CHUNK_BATCHES, o * P : (o + 1) * P, :
-                    ].rearrange("b m s -> m b s"),
-                    in_=totals[o][:],
-                )
+        def store(node, chunk, o, total):
+            nc.sync.dma_start(
+                out=result[
+                    node, chunk * CHUNK_BATCHES : (chunk + 1) * CHUNK_BATCHES, o * P : (o + 1) * P, :
+                ].rearrange("b m s -> m b s"),
+                in_=total,
+            )
 
         def finish(open_stage):
             node, chunk, conv, accs, others = open_stage
-            totals = norm_relu(conv, accs, "total")
-            if others is not None:
-                for o in range(O_TILES):
-                    nc.vector.tensor_add(out=totals[o][:], in0=totals[o][:], in1=others[o][:])
-            return node, chunk, totals
+            for o in range(O_TILES):
+                if o % 2 == 0:
+                    totals = keep.tile(
+                        [P, 2, CHUNK_BATCHES, PIXELS], F32, name="totals", tag="raw_1", bufs=RAW_TILES[1]
+                    )
+                total = totals[:, o % 2]
+                norm_relu(conv, o, accs[o], total)
+                if others is not None:
+                    nc.vector.tensor_add(out=total, in0=total, in1=others[:, o])
+                store(node, chunk, o, total)
 
-        open_stage = None
+        def nothing():
+            return None
+
+        finish_previous = nothing
+        shared = regroup_shared(stages[0])
         for i in range(len(stages)):
             chunk, node, conv, own, half = stages[i]
-            if 0 < i <= CHUNKS:
-                quantise_group("upper", i - 1)
-            if i < CHUNKS:
-                by_pixels[i] = turn_upper(i)
             others = None
+            for name, grouped in shared:
+                quantise(grouped, name, chunk, 0)
             if half is not None:
-                quantise_group(half, chunk)
-                quantise_group("full1", chunk)
-            finished = finish(open_stage) if open_stage is not None else None
+                decomposed = convolve("decomp", chunk, ("full1", half), ())
+            prepare(own, chunk, finish_previous)
+            shared = regroup_shared(stages[i + 1]) if i + 1 < len(stages) else []
             if half is not None:
-                others = norm_relu("decomp", convolve("decomp", chunk, ("full1", half), ()), "other")
-            if finished is not None:
-                store(*finished)
-            for name in own:
-                quantise_group(name, chunk)
+                others = stage_pool.tile([P, O_TILES, CHUNK_BATCHES, PIXELS], F32, name="others", bufs=1)
+                for o in range(O_TILES):
+                    norm_relu("decomp", o, decomposed[o], others[:, o])
             concatenation = own + ((half,) if half is not None else ())
-            accs = convolve(conv, chunk, concatenation, (half,))
-            open_stage = (node, chunk, conv, accs, others)
-        store(*finish(open_stage))
+            open_stage = (node, chunk, conv, convolve(conv, chunk, concatenation, (half,)), others)
+            finish_previous = lambda stage=open_stage: finish(stage)
+        finish_previous()

@@ -23,7 +23,11 @@ CHUNK_COLS = CHUNK_BATCHES * PIXELS
 QUADRANTS = 4
 LIVE_ROWS = 4
 RUN = 4
-RAW_TILES = {1: 12, 2: 2, 4: 2}
+SINGLE_UNITS = 12
+JOINT_PASSES = 6
+GROUPED_BUFS = 3
+WEIGHTS_BEHIND = 1
+ADD_LAG = 3
 EPS = 1e-5
 BN_ROWS = 4
 
@@ -56,14 +60,14 @@ def tile_gnn_pa_kernel(
     result = out.rearrange("n b c y x -> n b c (y x)")
 
     groups = {
-        "full0": (fulls[0],),
-        "half0": (halves[0],),
-        "part0": (parts[0],),
-        "full1": (fulls[1],),
-        "half1": (halves[1],),
-        "half2": (halves[2],),
-        "lower": (parts[5], parts[6]),
-        "upper": (parts[1], parts[2], parts[3], parts[4]),
+        "full0": fulls[0:1],
+        "half0": halves[0:1],
+        "part0": parts[0:1],
+        "full1": fulls[1:2],
+        "half1": halves[1:2],
+        "half2": halves[2:3],
+        "lower": parts[5:7],
+        "upper": parts[1:5],
     }
     convolutions = {
         "bg": (W_bg_h_words, W_bg_h_scales, bn_bg_h),
@@ -72,17 +76,21 @@ def tile_gnn_pa_kernel(
         "comp_u": (W_comp_u_words, W_comp_u_scales, bn_comp_u),
     }
     conv_names = list(convolutions)
+    by_scalar = (("half0", 0), ("half1", 0), ("half2", 0), ("upper", 3))
 
     node_stages = (
         (0, "bg", ("full0", "half0", "part0"), None),
         (2, "comp_l", ("lower",), "half2"),
         (1, "comp_u", ("upper",), "half1"),
     )
-    stages = [(0,) + s for s in node_stages] + [(1,) + s for s in reversed(node_stages)]
+    stages = [(chunk,) + s for s in node_stages for chunk in range(CHUNKS)]
+
+    def passes_of(name):
+        return groups[name].shape[0]
 
     with ExitStack() as ctx:
         keep = ctx.enter_context(tc.tile_pool(name="keep", bufs=1))
-        stage_pool = ctx.enter_context(tc.tile_pool(name="stage", bufs=4))
+        stage_pool = ctx.enter_context(tc.tile_pool(name="stage", bufs=GROUPED_BUFS))
         psum = ctx.enter_context(tc.psum_pool(name="psum", bufs=8))
         ctx.enter_context(tc.manual_schedule())
 
@@ -107,8 +115,8 @@ def tile_gnn_pa_kernel(
         nc.vector.memset(warm[:], 1.0)
         nc.scalar.sqrt(out=warm[:], in_=warm[:])
 
-        def load_weights(conv):
-            words, scales = convolutions[conv][0], convolutions[conv][1]
+        def load_planes(conv):
+            scales = convolutions[conv][1]
             for quadrant in range(QUADRANTS):
                 nc.sync.dma_start(
                     out=w_planes[conv][32 * quadrant : 32 * quadrant + LIVE_ROWS].bitcast(I32),
@@ -116,42 +124,73 @@ def tile_gnn_pa_kernel(
                     .rearrange("g r n -> r g n")
                     .bitcast(I32),
                 )
-            nc.sync.dma_start(out=w_words[conv][:], in_=words.rearrange("g p n t -> p g (n t)").bitcast(I32))
 
-        def load_group(name, chunk):
-            nodes = groups[name]
-            n = len(nodes)
-            raw = keep.tile(
-                [P, n, CHUNK_BATCHES, n, (PACK // n) * PIXELS],
-                BF16,
-                name="raw_%s_%d" % (name, chunk),
-                tag="raw_%d" % n,
-                bufs=RAW_TILES[n],
+        def load_words(conv, k):
+            nc.sync.dma_start(
+                out=w_words[conv][:, k, :],
+                in_=convolutions[conv][0][k].rearrange("p n t -> p (n t)").bitcast(I32),
             )
-            for j in range(n):
-                nc.sync.dma_start(
-                    out=raw[:, j],
-                    in_=nodes[j][chunk * CHUNK_BATCHES : (chunk + 1) * CHUNK_BATCHES].rearrange(
-                        "b (g p e) s -> p b g (e s)", g=n, p=P
-                    ),
-                )
-            return raw
 
         raws = {}
-        loaded_weights = set()
+        load_order = []
 
-        def load_step(chunk, names, conv):
-            for name in names:
-                if (name, chunk) not in raws:
-                    raws[name, chunk] = load_group(name, chunk)
-                if conv not in loaded_weights:
-                    load_weights(conv)
-                    loaded_weights.add(conv)
+        def load_unit(name, g, chunk):
+            n = passes_of(name)
+            width = CHANNELS // n
+            channels = groups[name][:, :, g * width : (g + 1) * width, :]
+            if n == 1:
+                raw = keep.tile([P, n, CHUNK_BATCHES, PACK * PIXELS], BF16, name="raw_1", tag="raw_1", bufs=SINGLE_UNITS)
+                nc.sync.dma_start(
+                    out=raw[:],
+                    in_=channels[:, chunk * CHUNK_BATCHES : (chunk + 1) * CHUNK_BATCHES].rearrange(
+                        "n b (p e) s -> p n b (e s)", p=P
+                    ),
+                )
+                raws[name, g, chunk] = raw[:]
+                load_order.append((name, g, chunk))
+            else:
+                raw = keep.tile([P, n, BATCH, (PACK // n) * PIXELS], BF16, name="raw_n", tag="raw_n", bufs=JOINT_PASSES)
+                nc.sync.dma_start(out=raw[:], in_=channels.rearrange("n b (p e) s -> p n b (e s)", p=P))
+                for c in range(CHUNKS):
+                    raws[name, g, c] = raw[:, :, c * CHUNK_BATCHES : (c + 1) * CHUNK_BATCHES, :]
 
-        for chunk, node, conv, own, half in stages:
-            if half is not None:
-                load_step(chunk, (half, "full1"), "decomp")
-            load_step(chunk, own, conv)
+        def concatenation(conv, half):
+            names = {
+                "bg": ("full0", "half0", "part0"),
+                "decomp": ("full1", half),
+                "comp_l": ("lower", half),
+                "comp_u": ("upper", half),
+            }[conv]
+            return [(name, g) for name in names for g in range(passes_of(name))]
+
+        have_planes = set()
+
+        def stage_convolutions(i):
+            chunk, node, conv, own, half = stages[i]
+            return ([] if half is None else [("decomp", half)]) + [(conv, half)]
+
+        def load_units(i):
+            chunk = stages[i][0]
+            units = [u for conv, half in stage_convolutions(i) for u in concatenation(conv, half)]
+            if stages[i][2] != "bg":
+                units = [u for u in units if u in by_scalar] + [u for u in units if u not in by_scalar]
+            for name, g in units:
+                if (name, g, chunk) not in raws:
+                    load_unit(name, g, chunk)
+
+        def load_weights(i):
+            for conv, half in stage_convolutions(i):
+                if conv not in have_planes:
+                    have_planes.add(conv)
+                    load_planes(conv)
+                    for k in range(convolutions[conv][0].shape[0]):
+                        load_words(conv, k)
+
+        for i in range(len(stages) + WEIGHTS_BEHIND):
+            if i < len(stages):
+                load_units(i)
+            if i >= WEIGHTS_BEHIND:
+                load_weights(i - WEIGHTS_BEHIND)
 
         identity = keep.tile([P, P], BF16, name="identity")
         make_identity(nc, identity[:])
@@ -171,137 +210,213 @@ def tile_gnn_pa_kernel(
         nc.vector.tensor_mul(out=bn_shift[:], in0=mean, in1=bn_scale[:])
         nc.vector.tensor_sub(out=bn_shift[:], in0=beta, in1=bn_shift[:])
 
+        grouped = {}
         codes = {}
         planes = {}
-        for chunk in range(CHUNKS):
-            for name in groups:
-                shape = [P, len(groups[name]), CHUNK_COLS]
-                codes[name, chunk] = keep.tile(shape, U32, name="codes_%s_%d" % (name, chunk), align_bytes=64)
-                planes[name, chunk] = keep.tile(shape, U8, name="planes_%s_%d" % (name, chunk), align_bytes=64)
+        accs = {}
+        others = {}
+        totals = {}
 
-        def regroup(name, chunk, g, tag):
-            n = len(groups[name])
-            raw = raws[name, chunk][:, :, :, g, :]
-            grouped = stage_pool.tile(
-                [P, CHUNK_BATCHES, PIXELS, PACK], BF16, name=tag, tag=tag, bufs=3, align_bytes=64
-            )
-            if tag == "by_scalar":
+        def regroup(unit):
+            name, g, chunk = unit
+            n = passes_of(name)
+            raw = raws[unit]
+            tag = "by_scalar" if (name, g) in by_scalar else "by_vector"
+            tile = stage_pool.tile([P, CHUNK_BATCHES, PIXELS, PACK], BF16, name=tag, tag=tag, align_bytes=64)
+            grouped[unit] = tile
+            if (name, g) in by_scalar:
                 nc.scalar.copy(
-                    out=grouped[:].rearrange("p b s (e j) -> p b s e j", j=n),
+                    out=tile[:].rearrange("p b s (e j) -> p b s e j", j=n),
                     in_=raw.rearrange("p j b (e s) -> p b s e j", s=PIXELS),
                 )
             elif n == 2:
                 nc.vector.tensor_copy(
-                    out=grouped[:].rearrange("p b s (e j) -> p b s e j", j=n),
+                    out=tile[:].rearrange("p b s (e j) -> p b s e j", j=n),
                     in_=raw.rearrange("p j b (e s) -> p b s e j", s=PIXELS),
                 )
             else:
                 nc.vector.tensor_copy(
-                    out=grouped[:].rearrange("p b (c i) (e j) -> p b c e j i", i=RUN, j=n),
+                    out=tile[:].rearrange("p b (c i) (e j) -> p b c e j i", i=RUN, j=n),
                     in_=raw.rearrange("p j b (e c i) -> p b c e j i", e=PACK // n, i=RUN),
                 )
-            return grouped
 
-        def quantise(grouped, name, chunk, g):
+        def quantise(unit):
+            codes[unit] = keep.tile([P, CHUNK_COLS], U32, name="codes_%s_%d_%d" % unit, align_bytes=64)
+            planes[unit] = keep.tile([P, CHUNK_COLS], U8, name="planes_%s_%d_%d" % unit, align_bytes=64)
             nc.vector.quantize_mx(
-                out=codes[name, chunk][:, g, :].bitcast(FP8X4),
-                scales=planes[name, chunk][:, g, :],
-                in_=grouped[:].rearrange("p b s t -> p (b s t)"),
+                out=codes[unit][:].bitcast(FP8X4),
+                scales=planes[unit][:],
+                in_=grouped[unit][:].rearrange("p b s t -> p (b s t)"),
             )
 
-        def prepare(names, chunk, between):
-            passes = [(name, g) for name in names for g in range(len(groups[name]))]
-            tiles = []
-            for k in range(len(passes) + 1):
-                if k < len(passes):
-                    tiles.append(regroup(passes[k][0], chunk, passes[k][1], "by_vector"))
-                if k == 0:
-                    between()
-                else:
-                    quantise(tiles[k - 1], passes[k - 1][0], chunk, passes[k - 1][1])
+        def multiply(inst, k, unit, first, last):
+            conv = inst[0]
+            if first:
+                accs[inst] = [psum.tile([P, CHUNK_COLS], F32, name="acc", tag="acc") for o in range(O_TILES)]
+            for o in range(O_TILES):
+                nc.tensor.matmul_mx(
+                    out=accs[inst][o][:],
+                    lhsT=w_words[conv][:, k, o * P : (o + 1) * P].bitcast(FP8X4),
+                    lhsT_scale=w_planes[conv][:, k, o * P : (o + 1) * P],
+                    rhs=codes[unit][:].bitcast(FP8X4),
+                    rhs_scale=planes[unit][:],
+                    start=first,
+                    stop=last,
+                )
 
-        seen = set()
-
-        def regroup_shared(stage):
-            chunk, node, conv, own, half = stage
-            tiles = []
-            if half is not None:
-                for name in (half, "full1"):
-                    if (name, chunk) not in seen:
-                        seen.add((name, chunk))
-                        tiles.append((name, regroup(name, chunk, 0, "by_scalar")))
-            return tiles
-
-        def convolve(conv, chunk, concatenation, first_names):
-            pairs = []
-            for name in concatenation:
-                for g in range(len(groups[name])):
-                    pairs.append((name not in first_names, len(pairs), name, g))
-            pairs = sorted(pairs)
-            accs = [psum.tile([P, CHUNK_COLS], F32, name="acc", tag="acc") for o in range(O_TILES)]
-            for late, k, name, g in pairs:
-                for o in range(O_TILES):
-                    nc.tensor.matmul_mx(
-                        out=accs[o][:],
-                        lhsT=w_words[conv][:, k, o * P : (o + 1) * P].bitcast(FP8X4),
-                        lhsT_scale=w_planes[conv][:, k, o * P : (o + 1) * P],
-                        rhs=codes[name, chunk][:, g, :].bitcast(FP8X4),
-                        rhs_scale=planes[name, chunk][:, g, :],
-                        start=((late, k, name, g) == pairs[0]),
-                        stop=((late, k, name, g) == pairs[-1]),
-                    )
-            return accs
-
-        def norm_relu(conv, o, acc, branch):
-            i = conv_names.index(conv)
+        def norm_relu(inst, o, branch):
+            i = conv_names.index(inst[0])
             nc.scalar.activation(
                 out=branch.rearrange("p b s -> p (b s)"),
-                in_=acc[:],
+                in_=accs[inst][o][:],
                 func=RELU,
                 bias=bn_shift[:, i, o : o + 1],
                 scale=bn_scale[:, i, o : o + 1],
             )
 
-        def store(node, chunk, o, total):
+        def empty_decomposition(inst, o):
+            if o == 0:
+                others[inst] = stage_pool.tile([P, O_TILES, CHUNK_BATCHES, PIXELS], F32, name="others", bufs=2)
+            norm_relu(inst, o, others[inst][:, o])
+
+        def empty_own(inst, o):
+            if o % 2 == 0:
+                totals[inst, o // 2] = keep.tile(
+                    [P, 2, CHUNK_BATCHES, PIXELS], F32, name="totals", tag="raw_1", bufs=SINGLE_UNITS
+                )
+            norm_relu(inst, o, totals[inst, o // 2][:, o % 2])
+
+        def add_branches(inst, other, o):
+            total = totals[inst, o // 2][:, o % 2]
+            nc.vector.tensor_add(out=total, in0=total, in1=others[other][:, o])
+
+        def store(inst, node, o):
+            chunk = inst[1]
             nc.sync.dma_start(
                 out=result[
                     node, chunk * CHUNK_BATCHES : (chunk + 1) * CHUNK_BATCHES, o * P : (o + 1) * P, :
                 ].rearrange("b m s -> m b s"),
-                in_=total,
+                in_=totals[inst, o // 2][:, o % 2],
             )
 
-        def finish(open_stage):
-            node, chunk, conv, accs, others = open_stage
-            for o in range(O_TILES):
-                if o % 2 == 0:
-                    totals = keep.tile(
-                        [P, 2, CHUNK_BATCHES, PIXELS], F32, name="totals", tag="raw_1", bufs=RAW_TILES[1]
+        vector, scalar, tensor, sync = [], [], [], []
+
+        def stage_units(i):
+            chunk, node, conv, own, half = stages[i]
+            names = (() if half is None else (half, "full1")) + own
+            return [(name, g, chunk) for name in names for g in range(passes_of(name))]
+
+        seen = set()
+        fresh = []
+        for i in range(len(stages)):
+            fresh.append([u for u in stage_units(i) if u not in seen])
+            for unit in fresh[i]:
+                seen.add(unit)
+
+        rings = {"by_vector": [], "by_scalar": []}
+
+        def copy_entry(unit):
+            tag = "by_scalar" if unit[:2] in by_scalar else "by_vector"
+            ring = rings[tag]
+            needs = [("quantise", ring[-GROUPED_BUFS])] if len(ring) >= GROUPED_BUFS else []
+            ring.append(unit)
+            return (("copy", unit), needs, lambda: regroup(unit))
+
+        def quantise_entry(unit):
+            return (("quantise", unit), [("copy", unit)], lambda: quantise(unit))
+
+        emptied = []
+
+        def convolve(inst, half, kind):
+            conv, chunk = inst[0], inst[1]
+            units = concatenation(conv, half)
+            order = sorted(range(len(units)), key=lambda k: (units[k] not in by_scalar or conv == "bg", k))
+            for position in range(len(order)):
+                k = order[position]
+                unit = units[k] + (chunk,)
+                needs = [("quantise", unit)]
+                if position == 0 and len(emptied) >= 2:
+                    needs = needs + emptied[-2]
+                tensor.append(
+                    (
+                        ("multiply", inst, k),
+                        needs,
+                        lambda k=k, unit=unit, a=(position == 0), z=(position == len(order) - 1): multiply(
+                            inst, k, unit, a, z
+                        ),
                     )
-                total = totals[:, o % 2]
-                norm_relu(conv, o, accs[o], total)
-                if others is not None:
-                    nc.vector.tensor_add(out=total, in0=total, in1=others[:, o])
-                store(node, chunk, o, total)
+                )
+            emptied.append([(kind, inst, o) for o in range(O_TILES)])
+            return ("multiply", inst, order[-1])
 
-        def nothing():
-            return None
-
-        finish_previous = nothing
-        shared = regroup_shared(stages[0])
+        vector_units = [u for i in range(len(stages)) for u in fresh[i] if u[:2] not in by_scalar]
+        vector.append(copy_entry(vector_units[0]))
+        for unit in fresh[0]:
+            if unit[:2] in by_scalar:
+                scalar.append(copy_entry(unit))
+        previous = []
+        adds = []
+        added = []
+        results = 0
         for i in range(len(stages)):
             chunk, node, conv, own, half = stages[i]
-            others = None
-            for name, grouped in shared:
-                quantise(grouped, name, chunk, 0)
+            own_inst = (conv, chunk, "own")
+            other_inst = ("decomp", chunk, half)
+            todo = [u for u in fresh[i] if u[:2] in by_scalar and conv != "bg"]
+            todo = todo + [u for u in fresh[i] if u not in todo]
+            for position in range(len(todo)):
+                unit = todo[position]
+                if unit in vector_units and vector_units.index(unit) + 1 < len(vector_units):
+                    vector.append(copy_entry(vector_units[vector_units.index(unit) + 1]))
+                vector.append(quantise_entry(unit))
+                if position + 1 == min(ADD_LAG, len(todo)):
+                    vector.extend(adds)
+            scalar.extend(previous)
+            if i + 1 < len(stages):
+                for unit in fresh[i + 1]:
+                    if unit[:2] in by_scalar:
+                        scalar.append(copy_entry(unit))
             if half is not None:
-                decomposed = convolve("decomp", chunk, ("full1", half), ())
-            prepare(own, chunk, finish_previous)
-            shared = regroup_shared(stages[i + 1]) if i + 1 < len(stages) else []
-            if half is not None:
-                others = stage_pool.tile([P, O_TILES, CHUNK_BATCHES, PIXELS], F32, name="others", bufs=1)
+                done = convolve(other_inst, half, "other")
                 for o in range(O_TILES):
-                    norm_relu("decomp", o, decomposed[o], others[:, o])
-            concatenation = own + ((half,) if half is not None else ())
-            open_stage = (node, chunk, conv, convolve(conv, chunk, concatenation, (half,)), others)
-            finish_previous = lambda stage=open_stage: finish(stage)
-        finish_previous()
+                    needs = [done] + (added[-2] if o == 0 and len(added) >= 2 else [])
+                    scalar.append((("other", other_inst, o), needs, lambda o=o, d=other_inst: empty_decomposition(d, o)))
+            done = convolve(own_inst, half, "own")
+            previous = []
+            adds = []
+            for o in range(O_TILES):
+                needs = [done]
+                if o % 2 == 0:
+                    needs.append(("copy", load_order[results]))
+                    results += 1
+                previous.append((("own", own_inst, o), needs, lambda o=o, t=own_inst: empty_own(t, o)))
+                ready = ("own", own_inst, o)
+                if half is not None:
+                    ready = ("add", own_inst, o)
+                    adds.append(
+                        (
+                            ready,
+                            [("own", own_inst, o), ("other", other_inst, o)],
+                            lambda o=o, t=own_inst, d=other_inst: add_branches(t, d, o),
+                        )
+                    )
+                sync.append((("store", own_inst, o), [ready], lambda o=o, t=own_inst, n=node: store(t, n, o)))
+            if adds:
+                added.append([entry[0] for entry in adds])
+        scalar.extend(previous)
+        vector.extend(adds)
+
+        programs = [vector, scalar, tensor, sync]
+        written = set()
+        heads = [0, 0, 0, 0]
+        moved = True
+        while moved:
+            moved = False
+            for e in range(len(programs)):
+                while heads[e] < len(programs[e]) and all(need in written for need in programs[e][heads[e]][1]):
+                    key, needs, call = programs[e][heads[e]]
+                    call()
+                    written.add(key)
+                    heads[e] += 1
+                    moved = True
+        assert all(heads[e] == len(programs[e]) for e in range(len(programs)))

@@ -24,10 +24,18 @@ QUADRANTS = 4
 LIVE_ROWS = 4
 RUN = 4
 SINGLE_UNITS = 12
-JOINT_PASSES = 6
+JOINT_PASSES = 2
+UPPER_PARTS = 4
+UPPER_LOADS = 4
+TURNS_A_BANK = 4
+TURN_BANKS = PIXELS // (2 * TURNS_A_BANK)
+PSUM_BANKS = 8
+UPPER_AHEAD = 2
+CODE_BUFS = 10
 GROUPED_BUFS = 3
 WEIGHTS_BEHIND = 1
-ADD_LAG = 3
+COPY_AHEAD = 3
+ADD_LAG = 5
 EPS = 1e-5
 BN_ROWS = 4
 
@@ -76,12 +84,12 @@ def tile_gnn_pa_kernel(
         "comp_u": (W_comp_u_words, W_comp_u_scales, bn_comp_u),
     }
     conv_names = list(convolutions)
-    by_scalar = (("half0", 0), ("half1", 0), ("half2", 0), ("upper", 3))
+    by_scalar = (("half0", 0), ("half1", 0), ("half2", 0))
 
     node_stages = (
-        (0, "bg", ("full0", "half0", "part0"), None),
-        (2, "comp_l", ("lower",), "half2"),
         (1, "comp_u", ("upper",), "half1"),
+        (2, "comp_l", ("lower",), "half2"),
+        (0, "bg", ("full0", "half0", "part0"), None),
     )
     stages = [(chunk,) + s for s in node_stages for chunk in range(CHUNKS)]
 
@@ -91,7 +99,7 @@ def tile_gnn_pa_kernel(
     with ExitStack() as ctx:
         keep = ctx.enter_context(tc.tile_pool(name="keep", bufs=1))
         stage_pool = ctx.enter_context(tc.tile_pool(name="stage", bufs=GROUPED_BUFS))
-        psum = ctx.enter_context(tc.psum_pool(name="psum", bufs=8))
+        psum = ctx.enter_context(tc.psum_pool(name="psum", bufs=PSUM_BANKS))
         ctx.enter_context(tc.manual_schedule())
 
         bn_rows = keep.tile([P, P], BF16, name="bn_rows")
@@ -154,6 +162,14 @@ def tile_gnn_pa_kernel(
                 for c in range(CHUNKS):
                     raws[name, g, c] = raw[:, :, c * CHUNK_BATCHES : (c + 1) * CHUNK_BATCHES, :]
 
+        up_raw = keep.tile([P, P, PIXELS], BF16, name="up_raw")
+        up_source = parts[1 : 1 + UPPER_PARTS].rearrange("n b (g q) s -> (n b g) q s", q=P)
+
+        def load_upper():
+            for piece in range(UPPER_LOADS):
+                some = slice(piece * P // UPPER_LOADS, (piece + 1) * P // UPPER_LOADS)
+                nc.sync.dma_start(out=up_raw[:, some, :], in_=up_source[:, some, :])
+
         def concatenation(conv, half):
             names = {
                 "bg": ("full0", "half0", "part0"),
@@ -175,7 +191,7 @@ def tile_gnn_pa_kernel(
             if stages[i][2] != "bg":
                 units = [u for u in units if u in by_scalar] + [u for u in units if u not in by_scalar]
             for name, g in units:
-                if (name, g, chunk) not in raws:
+                if (name, g, chunk) not in raws and name != "upper":
                     load_unit(name, g, chunk)
 
         def load_weights(i):
@@ -186,7 +202,11 @@ def tile_gnn_pa_kernel(
                     for k in range(convolutions[conv][0].shape[0]):
                         load_words(conv, k)
 
+        first_upper = [i for i in range(len(stages)) if stages[i][2] == "comp_u"][0]
         for i in range(len(stages) + WEIGHTS_BEHIND):
+            if i == max(first_upper - UPPER_AHEAD, 0):
+                load_upper()
+                load_weights(first_upper)
             if i < len(stages):
                 load_units(i)
             if i >= WEIGHTS_BEHIND:
@@ -210,6 +230,40 @@ def tile_gnn_pa_kernel(
         nc.vector.tensor_mul(out=bn_shift[:], in0=mean, in1=bn_scale[:])
         nc.vector.tensor_sub(out=bn_shift[:], in0=beta, in1=bn_shift[:])
 
+        identity_words = keep.tile([P, P], F32, name="identity_words")
+        make_identity(nc, identity_words[:])
+        order_gbn = keep.tile([P, P], F32, name="order_gbn")
+        nc.vector.tensor_copy(
+            out=order_gbn[:].rearrange("p (g b n) -> p g b n", b=BATCH, n=UPPER_PARTS),
+            in_=identity_words[:].rearrange("p (n b g) -> p g b n", b=BATCH, n=UPPER_PARTS),
+        )
+        up_words = up_raw[:].rearrange("p q s -> p (q s)").bitcast(F32).rearrange("p (q w) -> p q w", q=P)
+        up_grouped = keep.tile([P, UPPER_PARTS * BATCH, PIXELS, PACK], BF16, name="up_grouped", align_bytes=64)
+        pixels_a_bank = 2 * TURNS_A_BANK
+        turned_banks = {}
+
+        def turn(bank):
+            turned_banks[bank] = psum.tile([P, TURNS_A_BANK, P], F32, name="turned", tag="acc")
+            for a in range(TURNS_A_BANK):
+                nc.tensor.transpose(
+                    turned_banks[bank][:, a, :], up_words[:, :, bank * TURNS_A_BANK + a], order_gbn[:]
+                )
+
+        def unturn(bank):
+            halves_in = (
+                turned_banks[bank][:]
+                .rearrange("p a x -> p (a x)")
+                .bitcast(BF16)
+                .rearrange("p (a x n l) -> p x a l n", a=TURNS_A_BANK, n=UPPER_PARTS, l=2)
+            )
+            halves_out = up_grouped[:, :, bank * pixels_a_bank : (bank + 1) * pixels_a_bank, :].rearrange(
+                "p x (a l) n -> p x a l n", l=2
+            )
+            if bank % 2 == 0:
+                nc.vector.tensor_copy(out=halves_out, in_=halves_in)
+            else:
+                nc.scalar.copy(out=halves_out, in_=halves_in)
+
         grouped = {}
         codes = {}
         planes = {}
@@ -223,7 +277,7 @@ def tile_gnn_pa_kernel(
             raw = raws[unit]
             tag = "by_scalar" if (name, g) in by_scalar else "by_vector"
             tile = stage_pool.tile([P, CHUNK_BATCHES, PIXELS, PACK], BF16, name=tag, tag=tag, align_bytes=64)
-            grouped[unit] = tile
+            grouped[unit] = tile[:]
             if (name, g) in by_scalar:
                 nc.scalar.copy(
                     out=tile[:].rearrange("p b s (e j) -> p b s e j", j=n),
@@ -241,12 +295,17 @@ def tile_gnn_pa_kernel(
                 )
 
         def quantise(unit):
-            codes[unit] = keep.tile([P, CHUNK_COLS], U32, name="codes_%s_%d_%d" % unit, align_bytes=64)
-            planes[unit] = keep.tile([P, CHUNK_COLS], U8, name="planes_%s_%d_%d" % unit, align_bytes=64)
+            tag = "_full1" if unit[0] == "full1" else ""
+            bufs = CHUNKS if unit[0] == "full1" else CODE_BUFS
+            codes[unit] = keep.tile([P, CHUNK_COLS], U32, name="codes" + tag, bufs=bufs, align_bytes=64)
+            planes[unit] = keep.tile([P, CHUNK_COLS], U8, name="planes" + tag, bufs=bufs, align_bytes=64)
+            if unit[0] == "upper":
+                first = unit[1] * BATCH + unit[2] * CHUNK_BATCHES
+                grouped[unit] = up_grouped[:, first : first + CHUNK_BATCHES, :, :]
             nc.vector.quantize_mx(
                 out=codes[unit][:].bitcast(FP8X4),
                 scales=planes[unit][:],
-                in_=grouped[unit][:].rearrange("p b s t -> p (b s t)"),
+                in_=grouped[unit].rearrange("p b s t -> p (b s t)"),
             )
 
         def multiply(inst, k, unit, first, last):
@@ -322,21 +381,36 @@ def tile_gnn_pa_kernel(
             ring.append(unit)
             return (("copy", unit), needs, lambda: regroup(unit))
 
-        def quantise_entry(unit):
-            return (("quantise", unit), [("copy", unit)], lambda: quantise(unit))
+        rank = {}
 
-        emptied = []
+        def quantise_entry(unit):
+            rank[unit] = len(rank)
+            needs = [("unturn", bank) for bank in range(TURN_BANKS)] if unit[0] == "upper" else [("copy", unit)]
+            return (("quantise", unit), needs, lambda: quantise(unit))
+
+        readers = {}
+
+        banks = [[]]
+
+        def take_banks(emptiers):
+            needs = []
+            for keys in emptiers:
+                if len(banks) >= PSUM_BANKS:
+                    needs.extend(banks[-PSUM_BANKS])
+                banks.append(keys)
+            return needs
 
         def convolve(inst, half, kind):
             conv, chunk = inst[0], inst[1]
             units = concatenation(conv, half)
-            order = sorted(range(len(units)), key=lambda k: (units[k] not in by_scalar or conv == "bg", k))
+            order = sorted(range(len(units)), key=lambda k: rank[units[k] + (chunk,)])
             for position in range(len(order)):
                 k = order[position]
                 unit = units[k] + (chunk,)
                 needs = [("quantise", unit)]
-                if position == 0 and len(emptied) >= 2:
-                    needs = needs + emptied[-2]
+                readers.setdefault(unit, []).append(("multiply", inst, k))
+                if position == 0:
+                    needs = needs + take_banks([[(kind, inst, o)] for o in range(O_TILES)])
                 tensor.append(
                     (
                         ("multiply", inst, k),
@@ -346,50 +420,88 @@ def tile_gnn_pa_kernel(
                         ),
                     )
                 )
-            emptied.append([(kind, inst, o) for o in range(O_TILES)])
             return ("multiply", inst, order[-1])
 
-        vector_units = [u for i in range(len(stages)) for u in fresh[i] if u[:2] not in by_scalar]
-        vector.append(copy_entry(vector_units[0]))
-        for unit in fresh[0]:
-            if unit[:2] in by_scalar:
-                scalar.append(copy_entry(unit))
-        previous = []
-        adds = []
+        def unturn_entries(parity):
+            return [
+                (("unturn", bank), [("turn", bank)], lambda bank=bank: unturn(bank))
+                for bank in range(parity, TURN_BANKS, 2)
+            ]
+
+        quantise_order = []
+        for i in range(len(stages)):
+            conv = stages[i][2]
+            first = [u for u in fresh[i] if u[0] == "upper" or (u[:2] in by_scalar and conv == "comp_l")]
+            rest = [u for u in fresh[i] if u not in first]
+            if conv == "comp_u":
+                rest = [u for u in rest if u[:2] not in by_scalar] + [u for u in rest if u[:2] in by_scalar]
+            quantise_order.extend(first + rest)
+        vector_units = [u for u in quantise_order if u[:2] not in by_scalar and u[0] != "upper"]
+
+        last_of_stage = {}
+        for i in range(len(stages)):
+            last_of_stage[max(quantise_order.index(u) for u in stage_units(i))] = i
+        stage_adds = {}
+        copies = 0
+        due = []
+        vector_slots = []
+        for position in range(len(quantise_order)):
+            while (
+                copies < len(vector_units)
+                and quantise_order.index(vector_units[copies]) <= position + COPY_AHEAD
+                and (copies < GROUPED_BUFS or quantise_order.index(vector_units[copies - GROUPED_BUFS]) < position)
+            ):
+                vector.append(copy_entry(vector_units[copies]))
+                copies += 1
+            if quantise_order[position] == ("upper", 0, 0):
+                vector.extend(unturn_entries(0))
+            vector.append(quantise_entry(quantise_order[position]))
+            if position in last_of_stage:
+                due.append((position + ADD_LAG, last_of_stage[position]))
+            for when, i in list(due):
+                if position >= when or position == len(quantise_order) - 1:
+                    vector.append(("adds of stage", i))
+                    due.remove((when, i))
+
+        def scalar_copies(i):
+            if i < len(stages):
+                scalar.extend([copy_entry(u) for u in fresh[i] if u[:2] in by_scalar])
+
+        if first_upper > 0:
+            scalar_copies(0)
+            scalar_copies(1)
         added = []
         results = 0
         for i in range(len(stages)):
             chunk, node, conv, own, half = stages[i]
             own_inst = (conv, chunk, "own")
             other_inst = ("decomp", chunk, half)
-            todo = [u for u in fresh[i] if u[:2] in by_scalar and conv != "bg"]
-            todo = todo + [u for u in fresh[i] if u not in todo]
-            for position in range(len(todo)):
-                unit = todo[position]
-                if unit in vector_units and vector_units.index(unit) + 1 < len(vector_units):
-                    vector.append(copy_entry(vector_units[vector_units.index(unit) + 1]))
-                vector.append(quantise_entry(unit))
-                if position + 1 == min(ADD_LAG, len(todo)):
-                    vector.extend(adds)
-            scalar.extend(previous)
-            if i + 1 < len(stages):
-                for unit in fresh[i + 1]:
-                    if unit[:2] in by_scalar:
-                        scalar.append(copy_entry(unit))
-            if half is not None:
-                done = convolve(other_inst, half, "other")
-                for o in range(O_TILES):
-                    needs = [done] + (added[-2] if o == 0 and len(added) >= 2 else [])
-                    scalar.append((("other", other_inst, o), needs, lambda o=o, d=other_inst: empty_decomposition(d, o)))
-            done = convolve(own_inst, half, "own")
-            previous = []
+            kinds = ["own"] if half is None else (["own", "other"] if conv == "comp_u" else ["other", "own"])
             adds = []
+            if i == first_upper:
+                for bank in range(TURN_BANKS):
+                    tensor.append((("turn", bank), take_banks([[("unturn", bank)]]), lambda bank=bank: turn(bank)))
+                scalar.extend(unturn_entries(1))
+                if i == 0:
+                    scalar_copies(0)
+                    scalar_copies(1)
+            for kind in kinds:
+                if kind == "other":
+                    done = convolve(other_inst, half, "other")
+                    for o in range(O_TILES):
+                        needs = [done] + (added[-2] if o == 0 and len(added) >= 2 else [])
+                        scalar.append(
+                            (("other", other_inst, o), needs, lambda o=o, d=other_inst: empty_decomposition(d, o))
+                        )
+                else:
+                    done = convolve(own_inst, half, "own")
+                    for o in range(O_TILES):
+                        needs = [done]
+                        if o % 2 == 0:
+                            needs.append(("copy", load_order[results]))
+                            results += 1
+                        scalar.append((("own", own_inst, o), needs, lambda o=o, t=own_inst: empty_own(t, o)))
             for o in range(O_TILES):
-                needs = [done]
-                if o % 2 == 0:
-                    needs.append(("copy", load_order[results]))
-                    results += 1
-                previous.append((("own", own_inst, o), needs, lambda o=o, t=own_inst: empty_own(t, o)))
                 ready = ("own", own_inst, o)
                 if half is not None:
                     ready = ("add", own_inst, o)
@@ -401,10 +513,18 @@ def tile_gnn_pa_kernel(
                         )
                     )
                 sync.append((("store", own_inst, o), [ready], lambda o=o, t=own_inst, n=node: store(t, n, o)))
+            stage_adds[i] = adds
             if adds:
                 added.append([entry[0] for entry in adds])
-        scalar.extend(previous)
-        vector.extend(adds)
+            scalar_copies(i + 2)
+        vector = [e for entry in vector for e in (stage_adds[entry[1]] if entry[0] == "adds of stage" else [entry])]
+
+        code_ring = []
+        for key, needs, call in vector:
+            if key[0] == "quantise" and key[1][0] != "full1":
+                if len(code_ring) >= CODE_BUFS:
+                    needs.extend(readers[code_ring[-CODE_BUFS]])
+                code_ring.append(key[1])
 
         programs = [vector, scalar, tensor, sync]
         written = set()

@@ -30,12 +30,12 @@ UPPER_LOADS = 4
 TURNS_A_BANK = 4
 TURN_BANKS = PIXELS // (2 * TURNS_A_BANK)
 PSUM_BANKS = 8
-UPPER_AHEAD = 2
+UPPER_AHEAD = 0
 CODE_BUFS = 10
 GROUPED_BUFS = 3
 WEIGHTS_BEHIND = 1
-COPY_AHEAD = 3
-ADD_LAG = 5
+COPY_AHEAD = 2
+ADD_LAG = 6
 EPS = 1e-5
 BN_ROWS = 4
 
@@ -87,9 +87,9 @@ def tile_gnn_pa_kernel(
     by_scalar = (("half0", 0), ("half1", 0), ("half2", 0))
 
     node_stages = (
+        (0, "bg", ("full0", "half0", "part0"), None),
         (1, "comp_u", ("upper",), "half1"),
         (2, "comp_l", ("lower",), "half2"),
-        (0, "bg", ("full0", "half0", "part0"), None),
     )
     stages = [(chunk,) + s for s in node_stages for chunk in range(CHUNKS)]
 
@@ -463,13 +463,15 @@ def tile_gnn_pa_kernel(
                     vector.append(("adds of stage", i))
                     due.remove((when, i))
 
-        def scalar_copies(i):
-            if i < len(stages):
+        regrouped_stages = []
+
+        def scalar_copies(i, turned):
+            if i < len(stages) and i not in regrouped_stages and (i < first_upper or turned):
+                regrouped_stages.append(i)
                 scalar.extend([copy_entry(u) for u in fresh[i] if u[:2] in by_scalar])
 
-        if first_upper > 0:
-            scalar_copies(0)
-            scalar_copies(1)
+        scalar_copies(0, False)
+        scalar_copies(1, False)
         added = []
         results = 0
         for i in range(len(stages)):
@@ -482,9 +484,8 @@ def tile_gnn_pa_kernel(
                 for bank in range(TURN_BANKS):
                     tensor.append((("turn", bank), take_banks([[("unturn", bank)]]), lambda bank=bank: turn(bank)))
                 scalar.extend(unturn_entries(1))
-                if i == 0:
-                    scalar_copies(0)
-                    scalar_copies(1)
+                scalar_copies(i, True)
+                scalar_copies(i + 1, True)
             for kind in kinds:
                 if kind == "other":
                     done = convolve(other_inst, half, "other")
@@ -516,7 +517,7 @@ def tile_gnn_pa_kernel(
             stage_adds[i] = adds
             if adds:
                 added.append([entry[0] for entry in adds])
-            scalar_copies(i + 2)
+            scalar_copies(i + 2, i >= first_upper)
         vector = [e for entry in vector for e in (stage_adds[entry[1]] if entry[0] == "adds of stage" else [entry])]
 
         code_ring = []

@@ -308,20 +308,33 @@ def tile_gnn_pa_kernel(
                 in_=grouped[unit].rearrange("p b s t -> p (b s t)"),
             )
 
-        def multiply(inst, k, unit, first, last):
+        def multiply_tile(inst, o, k, unit, first, last):
             conv = inst[0]
+            nc.tensor.matmul_mx(
+                out=accs[inst][o][:],
+                lhsT=w_words[conv][:, k, o * P : (o + 1) * P].bitcast(FP8X4),
+                lhsT_scale=w_planes[conv][:, k, o * P : (o + 1) * P],
+                rhs=codes[unit][:].bitcast(FP8X4),
+                rhs_scale=planes[unit][:],
+                start=first,
+                stop=last,
+            )
+
+        def take_accumulators(inst):
+            accs[inst] = [psum.tile([P, CHUNK_COLS], F32, name="acc", tag="acc") for o in range(O_TILES)]
+
+        def multiply(inst, k, unit, first, last):
             if first:
-                accs[inst] = [psum.tile([P, CHUNK_COLS], F32, name="acc", tag="acc") for o in range(O_TILES)]
+                take_accumulators(inst)
             for o in range(O_TILES):
-                nc.tensor.matmul_mx(
-                    out=accs[inst][o][:],
-                    lhsT=w_words[conv][:, k, o * P : (o + 1) * P].bitcast(FP8X4),
-                    lhsT_scale=w_planes[conv][:, k, o * P : (o + 1) * P],
-                    rhs=codes[unit][:].bitcast(FP8X4),
-                    rhs_scale=planes[unit][:],
-                    start=first,
-                    stop=last,
-                )
+                multiply_tile(inst, o, k, unit, first, last)
+
+        def multiply_by_tiles(inst, passes):
+            take_accumulators(inst)
+            for o in range(O_TILES):
+                for position in range(len(passes)):
+                    k, unit = passes[position]
+                    multiply_tile(inst, o, k, unit, position == 0, position == len(passes) - 1)
 
         def norm_relu(inst, o, branch):
             i = conv_names.index(inst[0])
@@ -400,10 +413,21 @@ def tile_gnn_pa_kernel(
                 banks.append(keys)
             return needs
 
+        last_convolution = (stages[-1][2], stages[-1][0], "own")
+
         def convolve(inst, half, kind):
             conv, chunk = inst[0], inst[1]
             units = concatenation(conv, half)
             order = sorted(range(len(units)), key=lambda k: rank[units[k] + (chunk,)])
+            if inst == last_convolution:
+                passes = [(k, units[k] + (chunk,)) for k in order]
+                key = ("multiply", inst, order[-1])
+                needs = take_banks([[(kind, inst, o)] for o in range(O_TILES)])
+                for k, unit in passes:
+                    needs.append(("quantise", unit))
+                    readers.setdefault(unit, []).append(key)
+                tensor.append((key, needs, lambda: multiply_by_tiles(inst, passes)))
+                return key
             for position in range(len(order)):
                 k = order[position]
                 unit = units[k] + (chunk,)

@@ -32,7 +32,7 @@ TURN_BANKS = PIXELS // (2 * TURNS_A_BANK)
 PSUM_BANKS = 8
 UPPER_AHEAD = 0
 CODE_BUFS = 10
-GROUPED_BUFS = 3
+GROUPED_BUFS = {"by_vector": 3, "by_scalar": 2, "by_gpsimd": 2}
 WEIGHTS_BEHIND = 1
 COPY_AHEAD = 2
 ADD_LAG = 6
@@ -84,7 +84,8 @@ def tile_gnn_pa_kernel(
         "comp_u": (W_comp_u_words, W_comp_u_scales, bn_comp_u),
     }
     conv_names = list(convolutions)
-    by_scalar = (("half0", 0), ("half1", 0), ("half2", 0))
+    by_scalar = (("half0", 0), ("half2", 0))
+    by_gpsimd = (("half1", 0),)
 
     node_stages = (
         (0, "bg", ("full0", "half0", "part0"), None),
@@ -98,7 +99,7 @@ def tile_gnn_pa_kernel(
 
     with ExitStack() as ctx:
         keep = ctx.enter_context(tc.tile_pool(name="keep", bufs=1))
-        stage_pool = ctx.enter_context(tc.tile_pool(name="stage", bufs=GROUPED_BUFS))
+        stage_pool = ctx.enter_context(tc.tile_pool(name="stage", bufs=2))
         psum = ctx.enter_context(tc.psum_pool(name="psum", bufs=PSUM_BANKS))
         ctx.enter_context(tc.manual_schedule())
 
@@ -189,7 +190,8 @@ def tile_gnn_pa_kernel(
             chunk = stages[i][0]
             units = [u for conv, half in stage_convolutions(i) for u in concatenation(conv, half)]
             if stages[i][2] != "bg":
-                units = [u for u in units if u in by_scalar] + [u for u in units if u not in by_scalar]
+                ahead = by_scalar + by_gpsimd
+                units = [u for u in units if u in ahead] + [u for u in units if u not in ahead]
             for name, g in units:
                 if (name, g, chunk) not in raws and name != "upper":
                     load_unit(name, g, chunk)
@@ -206,6 +208,9 @@ def tile_gnn_pa_kernel(
         for i in range(len(stages) + WEIGHTS_BEHIND):
             if i == max(first_upper - UPPER_AHEAD, 0):
                 load_upper()
+                for name, g in by_gpsimd:
+                    for c in range(CHUNKS):
+                        load_unit(name, g, c)
                 load_weights(first_upper)
             if i < len(stages):
                 load_units(i)
@@ -271,14 +276,30 @@ def tile_gnn_pa_kernel(
         others = {}
         totals = {}
 
+        def copier(unit):
+            if unit[:2] in by_gpsimd:
+                return "by_gpsimd"
+            return "by_scalar" if unit[:2] in by_scalar else "by_vector"
+
         def regroup(unit):
             name, g, chunk = unit
             n = passes_of(name)
             raw = raws[unit]
-            tag = "by_scalar" if (name, g) in by_scalar else "by_vector"
-            tile = stage_pool.tile([P, CHUNK_BATCHES, PIXELS, PACK], BF16, name=tag, tag=tag, align_bytes=64)
+            tag = copier(unit)
+            tile = stage_pool.tile(
+                [P, CHUNK_BATCHES, PIXELS, PACK], BF16, name=tag, tag=tag, bufs=GROUPED_BUFS[tag], align_bytes=64
+            )
             grouped[unit] = tile[:]
-            if (name, g) in by_scalar:
+            if tag == "by_gpsimd":
+                nc.gpsimd.tensor_scalar(
+                    out=tile[:].rearrange("p b s (e j) -> p b s e j", j=n),
+                    in0=raw.rearrange("p j b (e s) -> p b s e j", s=PIXELS),
+                    scalar1=1.0,
+                    scalar2=0.0,
+                    op0=mybir.AluOpType.mult,
+                    op1=mybir.AluOpType.add,
+                )
+            elif tag == "by_scalar":
                 nc.scalar.copy(
                     out=tile[:].rearrange("p b s (e j) -> p b s e j", j=n),
                     in_=raw.rearrange("p j b (e s) -> p b s e j", s=PIXELS),
@@ -385,12 +406,12 @@ def tile_gnn_pa_kernel(
             for unit in fresh[i]:
                 seen.add(unit)
 
-        rings = {"by_vector": [], "by_scalar": []}
+        rings = {"by_vector": [], "by_scalar": [], "by_gpsimd": []}
 
         def copy_entry(unit):
-            tag = "by_scalar" if unit[:2] in by_scalar else "by_vector"
+            tag = copier(unit)
             ring = rings[tag]
-            needs = [("quantise", ring[-GROUPED_BUFS])] if len(ring) >= GROUPED_BUFS else []
+            needs = [("quantise", ring[-GROUPED_BUFS[tag]])] if len(ring) >= GROUPED_BUFS[tag] else []
             ring.append(unit)
             return (("copy", unit), needs, lambda: regroup(unit))
 
@@ -458,9 +479,9 @@ def tile_gnn_pa_kernel(
             first = [u for u in fresh[i] if u[0] == "upper" or (u[:2] in by_scalar and conv == "comp_l")]
             rest = [u for u in fresh[i] if u not in first]
             if conv == "comp_u":
-                rest = [u for u in rest if u[:2] not in by_scalar] + [u for u in rest if u[:2] in by_scalar]
+                rest = [u for u in rest if copier(u) == "by_vector"] + [u for u in rest if copier(u) != "by_vector"]
             quantise_order.extend(first + rest)
-        vector_units = [u for u in quantise_order if u[:2] not in by_scalar and u[0] != "upper"]
+        vector_units = [u for u in quantise_order if copier(u) == "by_vector" and u[0] != "upper"]
 
         last_of_stage = {}
         for i in range(len(stages)):
@@ -473,7 +494,10 @@ def tile_gnn_pa_kernel(
             while (
                 copies < len(vector_units)
                 and quantise_order.index(vector_units[copies]) <= position + COPY_AHEAD
-                and (copies < GROUPED_BUFS or quantise_order.index(vector_units[copies - GROUPED_BUFS]) < position)
+                and (
+                    copies < GROUPED_BUFS["by_vector"]
+                    or quantise_order.index(vector_units[copies - GROUPED_BUFS["by_vector"]]) < position
+                )
             ):
                 vector.append(copy_entry(vector_units[copies]))
                 copies += 1
@@ -551,9 +575,10 @@ def tile_gnn_pa_kernel(
                     needs.extend(readers[code_ring[-CODE_BUFS]])
                 code_ring.append(key[1])
 
-        programs = [vector, scalar, tensor, sync]
+        pool_engine = [copy_entry(u) for u in quantise_order if copier(u) == "by_gpsimd"]
+        programs = [vector, scalar, tensor, sync, pool_engine]
         written = set()
-        heads = [0, 0, 0, 0]
+        heads = [0 for program in programs]
         moved = True
         while moved:
             moved = False

@@ -84,7 +84,7 @@ def tile_gnn_pa_kernel(
         "comp_u": (W_comp_u_words, W_comp_u_scales, bn_comp_u),
     }
     conv_names = list(convolutions)
-    by_scalar = (("half0", 0), ("half2", 0))
+    by_scalar = (("half0", 0), ("half2", 0), ("full1", 0))
     by_gpsimd = (("half1", 0),)
 
     node_stages = (
@@ -92,7 +92,7 @@ def tile_gnn_pa_kernel(
         (1, "comp_u", ("upper",), "half1"),
         (2, "comp_l", ("lower",), "half2"),
     )
-    stages = [(chunk,) + s for s in node_stages for chunk in range(CHUNKS)]
+    stages = [(chunk,) + node_stages[k] for k, chunk in ((1, 0), (1, 1), (0, 0), (0, 1), (2, 0), (2, 1))]
 
     def passes_of(name):
         return groups[name].shape[0]

@@ -36,6 +36,7 @@ GROUPED_BUFS = {"by_vector": 3, "by_scalar": 2, "by_gpsimd": 2}
 WEIGHTS_BEHIND = 1
 COPY_AHEAD = 2
 ADD_LAG = 6
+WEAVE_FROM = 3
 EPS = 1e-5
 BN_ROWS = 4
 
@@ -208,7 +209,7 @@ def tile_gnn_pa_kernel(
         for i in range(len(stages) + WEIGHTS_BEHIND):
             if i == max(first_upper - UPPER_AHEAD, 0):
                 load_upper()
-                for name, g in by_gpsimd:
+                for name, g in by_gpsimd + (("full1", 0),):
                     for c in range(CHUNKS):
                         load_unit(name, g, c)
                 load_weights(first_upper)
@@ -467,6 +468,14 @@ def tile_gnn_pa_kernel(
                 )
             return ("multiply", inst, order[-1])
 
+        def weave(emptyings, others):
+            woven_calls = []
+            for position in range(len(emptyings)):
+                woven_calls.append(emptyings[position])
+                if WEAVE_FROM <= position + 1 < WEAVE_FROM + len(others):
+                    woven_calls.append(others[position + 1 - WEAVE_FROM])
+            return woven_calls + others[max(len(emptyings) + 1 - WEAVE_FROM, 0) :]
+
         def unturn_entries(parity):
             return [
                 (("unturn", bank), [("turn", bank)], lambda bank=bank: unturn(bank))
@@ -481,6 +490,8 @@ def tile_gnn_pa_kernel(
             if conv == "comp_u":
                 rest = [u for u in rest if copier(u) == "by_vector"] + [u for u in rest if copier(u) != "by_vector"]
             quantise_order.extend(first + rest)
+        woven = [u for u in quantise_order if u[0] in ("half1", "full1")]
+        quantise_order = woven + [u for u in quantise_order if u not in woven]
         vector_units = [u for u in quantise_order if copier(u) == "by_vector" and u[0] != "upper"]
 
         last_of_stage = {}
@@ -501,9 +512,10 @@ def tile_gnn_pa_kernel(
             ):
                 vector.append(copy_entry(vector_units[copies]))
                 copies += 1
-            if quantise_order[position] == ("upper", 0, 0):
-                vector.extend(unturn_entries(0))
-            vector.append(quantise_entry(quantise_order[position]))
+            if position == 0:
+                vector.extend(weave(unturn_entries(0), [quantise_entry(u) for u in woven]))
+            if quantise_order[position] not in woven:
+                vector.append(quantise_entry(quantise_order[position]))
             if position in last_of_stage:
                 due.append((position + ADD_LAG, last_of_stage[position]))
             for when, i in list(due):
@@ -526,14 +538,16 @@ def tile_gnn_pa_kernel(
             chunk, node, conv, own, half = stages[i]
             own_inst = (conv, chunk, "own")
             other_inst = ("decomp", chunk, half)
-            kinds = ["own"] if half is None else (["own", "other"] if conv == "comp_u" else ["other", "own"])
+            kinds = ["own"] if half is None else ["other", "own"]
             adds = []
             if i == first_upper:
                 for bank in range(TURN_BANKS):
                     tensor.append((("turn", bank), take_banks([[("unturn", bank)]]), lambda bank=bank: turn(bank)))
-                scalar.extend(unturn_entries(1))
+                mark = len(scalar)
                 scalar_copies(i, True)
                 scalar_copies(i + 1, True)
+                early = scalar[mark:]
+                scalar = scalar[:mark] + weave(unturn_entries(1), early)
             for kind in kinds:
                 if kind == "other":
                     done = convolve(other_inst, half, "other")

from contextlib import ExitStack

import concourse.mybir as mybir
from concourse.masks import make_identity

F32 = mybir.dt.float32
BF16 = mybir.dt.bfloat16
I32 = mybir.dt.int32
U32 = mybir.dt.uint32
U8 = mybir.dt.uint8
FP8X4 = mybir.dt.float8_e4m3fn_x4
RELU = mybir.ActivationFunctionType.Relu

P = 128
PACK = 4
BATCH = 8
CHANNELS = 512
PIXELS = 128
O_TILES = CHANNELS // P
CHUNK_BATCHES = 4
CHUNKS = BATCH // CHUNK_BATCHES
CHUNK_COLS = CHUNK_BATCHES * PIXELS
QUADRANTS = 4
LIVE_ROWS = 4
RUN = 4
SINGLE_UNITS = 12
JOINT_PASSES = 2
UPPER_PARTS = 4
UPPER_LOADS = 4
TURNS_A_BANK = 4
TURN_BANKS = PIXELS // (2 * TURNS_A_BANK)
PSUM_BANKS = 8
UPPER_AHEAD = 0
CODE_BUFS = 10
GROUPED_BUFS = {"by_vector": 3, "by_scalar": 2, "by_gpsimd": 2}
WEIGHTS_BEHIND = 1
COPY_AHEAD = 2
ADD_LAG = 6
WEAVE_FROM = 3
EPS = 1e-5
BN_ROWS = 4

FLOPS = 2 * CHANNELS * (1536 + 2560 + 1536 + 1024 + 1024) * BATCH * PIXELS


def tile_gnn_pa_kernel(
    tc,
    p_nodes,
    h_nodes,
    f_nodes,
    W_decomp_full_words,
    W_decomp_full_scales,
    bn_decomp_full,
    W_comp_u_words,
    W_comp_u_scales,
    bn_comp_u,
    W_comp_l_words,
    W_comp_l_scales,
    bn_comp_l,
    W_bg_h_words,
    W_bg_h_scales,
    bn_bg_h,
    out,
):
    nc = tc.nc
    parts = p_nodes.rearrange("n b c y x -> n b c (y x)")
    halves = h_nodes.rearrange("n b c y x -> n b c (y x)")
    fulls = f_nodes.rearrange("n b c y x -> n b c (y x)")
    result = out.rearrange("n b c y x -> n b c (y x)")

    groups = {
        "full0": fulls[0:1],
        "half0": halves[0:1],
        "part0": parts[0:1],
        "full1": fulls[1:2],
        "half1": halves[1:2],
        "half2": halves[2:3],
        "lower": parts[5:7],
        "upper": parts[1:5],
    }
    convolutions = {
        "bg": (W_bg_h_words, W_bg_h_scales, bn_bg_h),
        "decomp": (W_decomp_full_words, W_decomp_full_scales, bn_decomp_full),
        "comp_l": (W_comp_l_words, W_comp_l_scales, bn_comp_l),
        "comp_u": (W_comp_u_words, W_comp_u_scales, bn_comp_u),
    }
    conv_names = list(convolutions)
    by_scalar = (("half0", 0), ("half2", 0), ("full1", 0))
    by_gpsimd = (("half1", 0),)

    node_stages = (
        (0, "bg", ("full0", "half0", "part0"), None),
        (1, "comp_u", ("upper",), "half1"),
        (2, "comp_l", ("lower",), "half2"),
    )
    stages = [(chunk,) + node_stages[k] for k, chunk in ((1, 0), (1, 1), (0, 0), (0, 1), (2, 0), (2, 1))]

    def passes_of(name):
        return groups[name].shape[0]

    with ExitStack() as ctx:
        keep = ctx.enter_context(tc.tile_pool(name="keep", bufs=1))
        stage_pool = ctx.enter_context(tc.tile_pool(name="stage", bufs=2))
        psum = ctx.enter_context(tc.psum_pool(name="psum", bufs=PSUM_BANKS))
        ctx.enter_context(tc.manual_schedule())

        bn_rows = keep.tile([P, P], BF16, name="bn_rows")
        nc.vector.memset(bn_rows[P // 2 :, :], 0.0)
        rows_per_bn = BN_ROWS * O_TILES
        for i in range(len(conv_names)):
            nc.scalar.dma_start(
                out=bn_rows[i * rows_per_bn : (i + 1) * rows_per_bn, :],
                in_=convolutions[conv_names[i]][2].rearrange("r (j m) -> (r j) m", m=P),
            )

        w_words = {}
        w_planes = {}
        for conv in conv_names:
            passes = convolutions[conv][0].shape[0]
            w_words[conv] = keep.tile([P, passes, CHANNELS], I32, name="words_" + conv, align_bytes=64)
            w_planes[conv] = keep.tile([P, passes, CHANNELS], U8, name="planes_" + conv, align_bytes=64)
            nc.vector.memset(w_planes[conv][:].bitcast(I32), 0)

        warm = keep.tile([P, 1], F32, name="warm")
        nc.vector.memset(warm[:], 1.0)
        nc.scalar.sqrt(out=warm[:], in_=warm[:])

        def load_planes(conv):
            scales = convolutions[conv][1]
            for quadrant in range(QUADRANTS):
                nc.sync.dma_start(
                    out=w_planes[conv][32 * quadrant : 32 * quadrant + LIVE_ROWS].bitcast(I32),
                    in_=scales[:, LIVE_ROWS * quadrant : LIVE_ROWS * (quadrant + 1), :]
                    .rearrange("g r n -> r g n")
                    .bitcast(I32),
                )

        def load_words(conv, k):
            nc.sync.dma_start(
                out=w_words[conv][:, k, :],
                in_=convolutions[conv][0][k].rearrange("p n t -> p (n t)").bitcast(I32),
            )

        raws = {}
        load_order = []

        def load_unit(name, g, chunk):
            n = passes_of(name)
            width = CHANNELS // n
            channels = groups[name][:, :, g * width : (g + 1) * width, :]
            if n == 1:
                raw = keep.tile([P, n, CHUNK_BATCHES, PACK * PIXELS], BF16, name="raw_1", tag="raw_1", bufs=SINGLE_UNITS)
                nc.sync.dma_start(
                    out=raw[:],
                    in_=channels[:, chunk * CHUNK_BATCHES : (chunk + 1) * CHUNK_BATCHES].rearrange(
                        "n b (p e) s -> p n b (e s)", p=P
                    ),
                )
                raws[name, g, chunk] = raw[:]
                load_order.append((name, g, chunk))
            else:
                raw = keep.tile([P, n, BATCH, (PACK // n) * PIXELS], BF16, name="raw_n", tag="raw_n", bufs=JOINT_PASSES)
                nc.sync.dma_start(out=raw[:], in_=channels.rearrange("n b (p e) s -> p n b (e s)", p=P))
                for c in range(CHUNKS):
                    raws[name, g, c] = raw[:, :, c * CHUNK_BATCHES : (c + 1) * CHUNK_BATCHES, :]

        up_raw = keep.tile([P, P, PIXELS], BF16, name="up_raw")
        up_source = parts[1 : 1 + UPPER_PARTS].rearrange("n b (g q) s -> (n b g) q s", q=P)

        def load_upper():
            for piece in range(UPPER_LOADS):
                some = slice(piece * P // UPPER_LOADS, (piece + 1) * P // UPPER_LOADS)
                nc.sync.dma_start(out=up_raw[:, some, :], in_=up_source[:, some, :])

        def concatenation(conv, half):
            names = {
                "bg": ("full0", "half0", "part0"),
                "decomp": ("full1", half),
                "comp_l": ("lower", half),
                "comp_u": ("upper", half),
            }[conv]
            return [(name, g) for name in names for g in range(passes_of(name))]

        have_planes = set()

        def stage_convolutions(i):
            chunk, node, conv, own, half = stages[i]
            return ([] if half is None else [("decomp", half)]) + [(conv, half)]

        def load_units(i):
            chunk = stages[i][0]
            units = [u for conv, half in stage_convolutions(i) for u in concatenation(conv, half)]
            if stages[i][2] != "bg":
                ahead = by_scalar + by_gpsimd
                units = [u for u in units if u in ahead] + [u for u in units if u not in ahead]
            for name, g in units:
                if (name, g, chunk) not in raws and name != "upper":
                    load_unit(name, g, chunk)

        def load_weights(i):
            for conv, half in stage_convolutions(i):
                if conv not in have_planes:
                    have_planes.add(conv)
                    load_planes(conv)
                    for k in range(convolutions[conv][0].shape[0]):
                        load_words(conv, k)

        first_upper = [i for i in range(len(stages)) if stages[i][2] == "comp_u"][0]
        for i in range(len(stages) + WEIGHTS_BEHIND):
            if i == max(first_upper - UPPER_AHEAD, 0):
                load_upper()
                for name, g in by_gpsimd + (("full1", 0),):
                    for c in range(CHUNKS):
                        load_unit(name, g, c)
                load_weights(first_upper)
            if i < len(stages):
                load_units(i)
            if i >= WEIGHTS_BEHIND:
                load_weights(i - WEIGHTS_BEHIND)

        identity = keep.tile([P, P], BF16, name="identity")
        make_identity(nc, identity[:])
        bn_turned = psum.tile([P, P], BF16, name="bn_turned", tag="acc")
        nc.tensor.transpose(bn_turned[:], bn_rows[:], identity[:])
        bn_cols = keep.tile([P, len(conv_names), BN_ROWS, O_TILES], F32, name="bn_cols")
        nc.vector.tensor_copy(
            out=bn_cols[:].rearrange("p i r j -> p (i r j)"), in_=bn_turned[:, : len(conv_names) * rows_per_bn]
        )
        gamma, beta, mean, var = [bn_cols[:, :, r, :] for r in range(BN_ROWS)]
        bn_scale = keep.tile([P, len(conv_names), O_TILES], F32, name="bn_scale")
        bn_shift = keep.tile([P, len(conv_names), O_TILES], F32, name="bn_shift")
        nc.vector.tensor_scalar_add(out=bn_scale[:], in0=var, scalar1=EPS)
        nc.scalar.sqrt(out=bn_scale[:], in_=bn_scale[:])
        nc.vector.reciprocal(out=bn_scale[:], in_=bn_scale[:])
        nc.vector.tensor_mul(out=bn_scale[:], in0=bn_scale[:], in1=gamma)
        nc.vector.tensor_mul(out=bn_shift[:], in0=mean, in1=bn_scale[:])
        nc.vector.tensor_sub(out=bn_shift[:], in0=beta, in1=bn_shift[:])

        identity_words = keep.tile([P, P], F32, name="identity_words")
        make_identity(nc, identity_words[:])
        order_gbn = keep.tile([P, P], F32, name="order_gbn")
        nc.vector.tensor_copy(
            out=order_gbn[:].rearrange("p (g b n) -> p g b n", b=BATCH, n=UPPER_PARTS),
            in_=identity_words[:].rearrange("p (n b g) -> p g b n", b=BATCH, n=UPPER_PARTS),
        )
        up_words = up_raw[:].rearrange("p q s -> p (q s)").bitcast(F32).rearrange("p (q w) -> p q w", q=P)
        up_grouped = keep.tile([P, UPPER_PARTS * BATCH, PIXELS, PACK], BF16, name="up_grouped", align_bytes=64)
        pixels_a_bank = 2 * TURNS_A_BANK
        turned_banks = {}

        def turn(bank):
            turned_banks[bank] = psum.tile([P, TURNS_A_BANK, P], F32, name="turned", tag="acc")
            for a in range(TURNS_A_BANK):
                nc.tensor.transpose(
                    turned_banks[bank][:, a, :], up_words[:, :, bank * TURNS_A_BANK + a], order_gbn[:]
                )

        def unturn(bank):
            halves_in = (
                turned_banks[bank][:]
                .rearrange("p a x -> p (a x)")
                .bitcast(BF16)
                .rearrange("p (a x n l) -> p x a l n", a=TURNS_A_BANK, n=UPPER_PARTS, l=2)
            )
            halves_out = up_grouped[:, :, bank * pixels_a_bank : (bank + 1) * pixels_a_bank, :].rearrange(
                "p x (a l) n -> p x a l n", l=2
            )
            if bank % 2 == 0:
                nc.vector.tensor_copy(out=halves_out, in_=halves_in)
            else:
                nc.scalar.copy(out=halves_out, in_=halves_in)

        grouped = {}
        codes = {}
        planes = {}
        accs = {}
        others = {}
        totals = {}

        def copier(unit):
            if unit[:2] in by_gpsimd:
                return "by_gpsimd"
            return "by_scalar" if unit[:2] in by_scalar else "by_vector"

        def regroup(unit):
            name, g, chunk = unit
            n = passes_of(name)
            raw = raws[unit]
            tag = copier(unit)
            tile = stage_pool.tile(
                [P, CHUNK_BATCHES, PIXELS, PACK], BF16, name=tag, tag=tag, bufs=GROUPED_BUFS[tag], align_bytes=64
            )
            grouped[unit] = tile[:]
            if tag == "by_gpsimd":
                nc.gpsimd.tensor_scalar(
                    out=tile[:].rearrange("p b s (e j) -> p b s e j", j=n),
                    in0=raw.rearrange("p j b (e s) -> p b s e j", s=PIXELS),
                    scalar1=1.0,
                    scalar2=0.0,
                    op0=mybir.AluOpType.mult,
                    op1=mybir.AluOpType.add,
                )
            elif tag == "by_scalar":
                nc.scalar.copy(
                    out=tile[:].rearrange("p b s (e j) -> p b s e j", j=n),
                    in_=raw.rearrange("p j b (e s) -> p b s e j", s=PIXELS),
                )
            elif n == 2:
                nc.vector.tensor_copy(
                    out=tile[:].rearrange("p b s (e j) -> p b s e j", j=n),
                    in_=raw.rearrange("p j b (e s) -> p b s e j", s=PIXELS),
                )
            else:
                nc.vector.tensor_copy(
                    out=tile[:].rearrange("p b (c i) (e j) -> p b c e j i", i=RUN, j=n),
                    in_=raw.rearrange("p j b (e c i) -> p b c e j i", e=PACK // n, i=RUN),
                )

        def quantise(unit):
            tag = "_full1" if unit[0] == "full1" else ""
            bufs = CHUNKS if unit[0] == "full1" else CODE_BUFS
            codes[unit] = keep.tile([P, CHUNK_COLS], U32, name="codes" + tag, bufs=bufs, align_bytes=64)
            planes[unit] = keep.tile([P, CHUNK_COLS], U8, name="planes" + tag, bufs=bufs, align_bytes=64)
            if unit[0] == "upper":
                first = unit[1] * BATCH + unit[2] * CHUNK_BATCHES
                grouped[unit] = up_grouped[:, first : first + CHUNK_BATCHES, :, :]
            nc.vector.quantize_mx(
                out=codes[unit][:].bitcast(FP8X4),
                scales=planes[unit][:],
                in_=grouped[unit].rearrange("p b s t -> p (b s t)"),
            )

        def multiply_tile(inst, o, k, unit, first, last):
            conv = inst[0]
            nc.tensor.matmul_mx(
                out=accs[inst][o][:],
                lhsT=w_words[conv][:, k, o * P : (o + 1) * P].bitcast(FP8X4),
                lhsT_scale=w_planes[conv][:, k, o * P : (o + 1) * P],
                rhs=codes[unit][:].bitcast(FP8X4),
                rhs_scale=planes[unit][:],
                start=first,
                stop=last,
            )

        def take_accumulators(inst):
            accs[inst] = [psum.tile([P, CHUNK_COLS], F32, name="acc", tag="acc") for o in range(O_TILES)]

        def multiply(inst, k, unit, first, last):
            if first:
                take_accumulators(inst)
            for o in range(O_TILES):
                multiply_tile(inst, o, k, unit, first, last)

        def multiply_by_tiles(inst, passes):
            take_accumulators(inst)
            for o in range(O_TILES):
                for position in range(len(passes)):
                    k, unit = passes[position]
                    multiply_tile(inst, o, k, unit, position == 0, position == len(passes) - 1)

        def norm_relu(inst, o, branch):
            i = conv_names.index(inst[0])
            nc.scalar.activation(
                out=branch.rearrange("p b s -> p (b s)"),
                in_=accs[inst][o][:],
                func=RELU,
                bias=bn_shift[:, i, o : o + 1],
                scale=bn_scale[:, i, o : o + 1],
            )

        def empty_decomposition(inst, o):
            if o == 0:
                others[inst] = stage_pool.tile([P, O_TILES, CHUNK_BATCHES, PIXELS], F32, name="others", bufs=2)
            norm_relu(inst, o, others[inst][:, o])

        def empty_own(inst, o):
            if o % 2 == 0:
                totals[inst, o // 2] = keep.tile(
                    [P, 2, CHUNK_BATCHES, PIXELS], F32, name="totals", tag="raw_1", bufs=SINGLE_UNITS
                )
            norm_relu(inst, o, totals[inst, o // 2][:, o % 2])

        def add_branches(inst, other, o):
            total = totals[inst, o // 2][:, o % 2]
            nc.vector.tensor_add(out=total, in0=total, in1=others[other][:, o])

        def store(inst, node, o):
            chunk = inst[1]
            nc.sync.dma_start(
                out=result[
                    node, chunk * CHUNK_BATCHES : (chunk + 1) * CHUNK_BATCHES, o * P : (o + 1) * P, :
                ].rearrange("b m s -> m b s"),
                in_=totals[inst, o // 2][:, o % 2],
            )

        vector, scalar, tensor, sync = [], [], [], []

        def stage_units(i):
            chunk, node, conv, own, half = stages[i]
            names = (() if half is None else (half, "full1")) + own
            return [(name, g, chunk) for name in names for g in range(passes_of(name))]

        seen = set()
        fresh = []
        for i in range(len(stages)):
            fresh.append([u for u in stage_units(i) if u not in seen])
            for unit in fresh[i]:
                seen.add(unit)

        rings = {"by_vector": [], "by_scalar": [], "by_gpsimd": []}

        def copy_entry(unit):
            tag = copier(unit)
            ring = rings[tag]
            needs = [("quantise", ring[-GROUPED_BUFS[tag]])] if len(ring) >= GROUPED_BUFS[tag] else []
            ring.append(unit)
            return (("copy", unit), needs, lambda: regroup(unit))

        rank = {}

        def quantise_entry(unit):
            rank[unit] = len(rank)
            needs = [("unturn", bank) for bank in range(TURN_BANKS)] if unit[0] == "upper" else [("copy", unit)]
            return (("quantise", unit), needs, lambda: quantise(unit))

        readers = {}

        banks = [[]]

        def take_banks(emptiers):
            needs = []
            for keys in emptiers:
                if len(banks) >= PSUM_BANKS:
                    needs.extend(banks[-PSUM_BANKS])
                banks.append(keys)
            return needs

        last_convolution = (stages[-1][2], stages[-1][0], "own")

        def convolve(inst, half, kind):
            conv, chunk = inst[0], inst[1]
            units = concatenation(conv, half)
            order = sorted(range(len(units)), key=lambda k: rank[units[k] + (chunk,)])
            if inst == last_convolution:
                passes = [(k, units[k] + (chunk,)) for k in order]
                key = ("multiply", inst, order[-1])
                needs = take_banks([[(kind, inst, o)] for o in range(O_TILES)])
                for k, unit in passes:
                    needs.append(("quantise", unit))
                    readers.setdefault(unit, []).append(key)
                tensor.append((key, needs, lambda: multiply_by_tiles(inst, passes)))
                return key
            for position in range(len(order)):
                k = order[position]
                unit = units[k] + (chunk,)
                needs = [("quantise", unit)]
                readers.setdefault(unit, []).append(("multiply", inst, k))
                if position == 0:
                    needs = needs + take_banks([[(kind, inst, o)] for o in range(O_TILES)])
                tensor.append(
                    (
                        ("multiply", inst, k),
                        needs,
                        lambda k=k, unit=unit, a=(position == 0), z=(position == len(order) - 1): multiply(
                            inst, k, unit, a, z
                        ),
                    )
                )
            return ("multiply", inst, order[-1])

        def weave(emptyings, others):
            woven_calls = []
            for position in range(len(emptyings)):
                woven_calls.append(emptyings[position])
                if WEAVE_FROM <= position + 1 < WEAVE_FROM + len(others):
                    woven_calls.append(others[position + 1 - WEAVE_FROM])
            return woven_calls + others[max(len(emptyings) + 1 - WEAVE_FROM, 0) :]

        def unturn_entries(parity):
            return [
                (("unturn", bank), [("turn", bank)], lambda bank=bank: unturn(bank))
                for bank in range(parity, TURN_BANKS, 2)
            ]

        quantise_order = []
        for i in range(len(stages)):
            conv = stages[i][2]
            first = [u for u in fresh[i] if u[0] == "upper" or (u[:2] in by_scalar and conv == "comp_l")]
            rest = [u for u in fresh[i] if u not in first]
            if conv == "comp_u":
                rest = [u for u in rest if copier(u) == "by_vector"] + [u for u in rest if copier(u) != "by_vector"]
            quantise_order.extend(first + rest)
        woven = [u for u in quantise_order if u[0] in ("half1", "full1")]
        quantise_order = woven + [u for u in quantise_order if u not in woven]
        vector_units = [u for u in quantise_order if copier(u) == "by_vector" and u[0] != "upper"]

        last_of_stage = {}
        for i in range(len(stages)):
            last_of_stage[max(quantise_order.index(u) for u in stage_units(i))] = i
        stage_adds = {}
        copies = 0
        due = []
        vector_slots = []
        for position in range(len(quantise_order)):
            while (
                copies < len(vector_units)
                and quantise_order.index(vector_units[copies]) <= position + COPY_AHEAD
                and (
                    copies < GROUPED_BUFS["by_vector"]
                    or quantise_order.index(vector_units[copies - GROUPED_BUFS["by_vector"]]) < position
                )
            ):
                vector.append(copy_entry(vector_units[copies]))
                copies += 1
            if position == 0:
                vector.extend(weave(unturn_entries(0), [quantise_entry(u) for u in woven]))
            if quantise_order[position] not in woven:
                vector.append(quantise_entry(quantise_order[position]))
            if position in last_of_stage:
                due.append((position + ADD_LAG, last_of_stage[position]))
            for when, i in list(due):
                if position >= when or position == len(quantise_order) - 1:
                    vector.append(("adds of stage", i))
                    due.remove((when, i))

        regrouped_stages = []

        def scalar_copies(i, turned):
            if i < len(stages) and i not in regrouped_stages and (i < first_upper or turned):
                regrouped_stages.append(i)
                scalar.extend([copy_entry(u) for u in fresh[i] if u[:2] in by_scalar])

        scalar_copies(0, False)
        scalar_copies(1, False)
        added = []
        results = 0
        for i in range(len(stages)):
            chunk, node, conv, own, half = stages[i]
            own_inst = (conv, chunk, "own")
            other_inst = ("decomp", chunk, half)
            kinds = ["own"] if half is None else ["other", "own"]
            adds = []
            if i == first_upper:
                for bank in range(TURN_BANKS):
                    tensor.append((("turn", bank), take_banks([[("unturn", bank)]]), lambda bank=bank: turn(bank)))
                mark = len(scalar)
                scalar_copies(i, True)
                scalar_copies(i + 1, True)
                early = scalar[mark:]
                scalar = scalar[:mark] + weave(unturn_entries(1), early)
            for kind in kinds:
                if kind == "other":
                    done = convolve(other_inst, half, "other")
                    for o in range(O_TILES):
                        needs = [done] + (added[-2] if o == 0 and len(added) >= 2 else [])
                        scalar.append(
                            (("other", other_inst, o), needs, lambda o=o, d=other_inst: empty_decomposition(d, o))
                        )
                else:
                    done = convolve(own_inst, half, "own")
                    for o in range(O_TILES):
                        needs = [done]
                        if o % 2 == 0:
                            needs.append(("copy", load_order[results]))
                            results += 1
                        scalar.append((("own", own_inst, o), needs, lambda o=o, t=own_inst: empty_own(t, o)))
            for o in range(O_TILES):
                ready = ("own", own_inst, o)
                if half is not None:
                    ready = ("add", own_inst, o)
                    adds.append(
                        (
                            ready,
                            [("own", own_inst, o), ("other", other_inst, o)],
                            lambda o=o, t=own_inst, d=other_inst: add_branches(t, d, o),
                        )
                    )
                sync.append((("store", own_inst, o), [ready], lambda o=o, t=own_inst, n=node: store(t, n, o)))
            stage_adds[i] = adds
            if adds:
                added.append([entry[0] for entry in adds])
            scalar_copies(i + 2, i >= first_upper)
        vector = [e for entry in vector for e in (stage_adds[entry[1]] if entry[0] == "adds of stage" else [entry])]

        code_ring = []
        for key, needs, call in vector:
            if key[0] == "quantise" and key[1][0] != "full1":
                if len(code_ring) >= CODE_BUFS:
                    needs.extend(readers[code_ring[-CODE_BUFS]])
                code_ring.append(key[1])

        pool_engine = [copy_entry(u) for u in quantise_order if copier(u) == "by_gpsimd"]
        programs = [vector, scalar, tensor, sync, pool_engine]
        written = set()
        heads = [0 for program in programs]
        moved = True
        while moved:
            moved = False
            for e in range(len(programs)):
                while heads[e] < len(programs[e]) and all(need in written for need in programs[e][heads[e]][1]):
                    key, needs, call = programs[e][heads[e]]
                    call()
                    written.add(key)
                    heads[e] += 1
                    moved = True
        assert all(heads[e] == len(programs[e]) for e in range(len(programs)))
